import numpy as np
import ml_dtypes


def mxq(x, axis, fmt="e4m3"):
    dtype, down = {"e4m3": (ml_dtypes.float8_e4m3fn, 7), "e5m2": (ml_dtypes.float8_e5m2, 14)}[fmt]
    v = np.moveaxis(np.asarray(x, np.float32).astype(ml_dtypes.bfloat16).astype(np.float64), axis, -1)
    blocks = v.reshape(v.shape[:-1] + (-1, 32))
    amax = np.abs(blocks).max(-1, keepdims=True)
    byte = np.maximum(np.where(amax > 0, np.frexp(amax)[1] - 1 + 127, 0) - down, 1)
    scale = np.exp2(byte - 127.0)
    codes = (blocks / scale).astype(np.float32).astype(dtype).astype(np.float64)
    return np.moveaxis((codes * scale).reshape(v.shape), -1, axis)


WIDE = False


def mx_kscale(k):
    if not WIDE:
        return np.ones(k)
    levels = np.array([10, -10, 5, -5, 0])
    if k % 512:
        return np.exp2(np.random.permutation(np.resize(levels, k // 32))).repeat(32)
    a = np.empty((k // 512, 16))
    for p in range(k // 512):
        a[p, :8] = np.random.permutation(np.resize(levels, 8))
        for g in range(8):
            far = levels[np.abs(levels - a[p, g]) >= 10]
            a[p, g + 8] = far[np.random.randint(len(far))]
    return np.exp2(a.ravel()).repeat(32)


BF16 = ml_dtypes.bfloat16


def bf(x):
    return np.asarray(x, np.float32).astype(BF16)


def f64(x):
    return np.asarray(x).astype(np.float64)


L, F, O, N, B, D = 2, 512, 512, 512, 1, 3
G = O + O + O
T = D * B * N


def sigmoid(v):
    return 1.0 / (1.0 + np.exp(-v))


def forward_parts(agg, x, wih, whh, bih, bhh, wh, bh):
    x = f64(x)
    h = x.transpose(1, 0, 2)[None]
    gi = f64(agg) @ f64(wih).T + f64(bih)
    gh = h @ f64(whh).T + f64(bhh)
    r = sigmoid(gi[..., :O] + gh[..., :O])
    z = sigmoid(gi[..., O:O + O] + gh[..., O:O + O])
    c = np.tanh(gi[..., O + O:] + r * gh[..., O + O:])
    hnew = (1.0 - z) * c + z * h
    u = np.maximum(hnew.sum(0).transpose(1, 0, 2), 0.0)
    t = np.maximum(x @ f64(wh) + f64(bh), 0.0)
    return {"y": u * t + x * (1.0 - t),
            "gates": np.concatenate([r, z, c], axis=-1),
            "hn": gh[0][..., O + O:],
            "t": t}


def setup_inputs():
    s = mx_kscale(N)
    u = mx_kscale(O)
    agg0 = bf(np.random.standard_normal((D, B, N, O)))
    x = bf(np.random.standard_normal((N, B, F)))
    wih0 = bf(np.random.standard_normal((G, O)) * 0.7 / np.sqrt(O))
    whh = bf(np.random.standard_normal((G, O)) * 0.7 / np.sqrt(O))
    bih = bf(np.random.standard_normal(G) * 0.3)
    bhh = bf(np.random.standard_normal(G) * 0.3)
    wh = bf(np.random.standard_normal((F, O)) * 0.5 / np.sqrt(F))
    bh = bf(0.3 + np.random.standard_normal(O) * 0.2)
    g = bf(np.random.standard_normal((N, B, O)) * np.exp2(np.random.randint(-6, 1, (N, B, 1))) * 16.0 / s[:, None, None] * u)
    p = forward_parts(agg0, x, wih0, whh, bih, bhh, wh, bh)
    return {"agg": bf(f64(agg0) * s[None, None, :, None]), "x": x,
            "wih": bf(f64(wih0) / np.tile(u, 3)[:, None]),
            "whh": whh, "bih": bih, "bhh": bhh, "wh": wh, "bh": bh,
            "gates": np.asarray(p["gates"], np.float32),
            "hn": np.asarray(p["hn"], np.float32),
            "t": np.asarray(p["t"], np.float32),
            "grad_out": g}


def reference(agg, x, wih, whh, bih, bhh, wh, bh, gates, hn, t, grad_out):
    h = f64(x).transpose(1, 0, 2)[None]
    gt = f64(gates)
    r, z, c = gt[..., :O], gt[..., O:O + O], gt[..., O + O:]
    hsum = ((1.0 - z) * c + z * h).sum(0)
    ds = np.where(hsum > 0.0, (f64(grad_out) * f64(t)).transpose(1, 0, 2), 0.0)[None]
    dc = ds * (1.0 - z) * (1.0 - c * c)
    dr = dc * f64(hn)[None] * r * (1.0 - r)
    dz = ds * (h - c) * z * (1.0 - z)
    dgi = np.concatenate([dr, dz, dc], axis=-1).reshape(T, G)
    a = f64(agg).reshape(T, O)
    dagg = mxq(dgi, 1, "e5m2") @ mxq(f64(wih), 0, "e4m3")
    dwih = mxq(dgi, 0, "e5m2").T @ mxq(a, 0, "e4m3")
    return dagg.reshape(D, B, N, O), dwih

@@ -1,0 +1,327 @@
+from contextlib import ExitStack
+
+import concourse.masks as masks
+import concourse.mybir as mybir
+
+F32 = mybir.dt.float32
+BF16 = mybir.dt.bfloat16
+U32 = mybir.dt.uint32
+U8 = mybir.dt.uint8
+E4M3X4 = mybir.dt.float8_e4m3fn_x4
+E5M2X4 = mybir.dt.float8_e5m2_x4
+ALU = mybir.AluOpType
+ACT = mybir.ActivationFunctionType
+
+P = 128
+J = 4
+W = 512
+ND = 3
+NG = 3
+ROW = J * W
+GATE_R, GATE_Z, GATE_C = 0, 1, 2
+
+FLOPS = 2 * 2 * (ND * W) * (NG * W) * W
+BYTES = 2 * (ND * W * W + W * W + NG * W * W + W * W) + 4 * (ND * W * NG * W + 2 * W * W) + 4 * 2 * ND * W * W
+
+
+def tile_graphconvolution_pb_v_kernel(
+    tc, agg, x, wih, whh, bih, bhh, wh, bh, gates, hn, t, grad_out, out_0, out_1
+):
+    nc = tc.nc
+
+    gates_v = gates[:, 0, :, :].rearrange("d (p j) f -> p d j f", j=J)
+    x_v = x[:, 0, :].rearrange("(p j) w -> p j w", j=J)
+    g_v = grad_out[:, 0, :].rearrange("(p j) w -> p j w", j=J)
+    t_v = t[:, 0, :].rearrange("(p j) w -> p j w", j=J)
+    hn_v = hn[0, :, :].rearrange("(p j) w -> p j w", j=J)
+    agg_v = agg[:, 0, :, :].rearrange("d (p j) w -> d p j w", j=J)
+    wih_v = wih.rearrange("(g p j) c -> g p j c", g=NG, j=J)
+    out0_v = out_0[:, 0, :, :].rearrange("d (p j) w -> d p j w", j=J)
+    out1_v = out_1.rearrange("(m p) c -> m p c", p=P)
+
+    with ExitStack() as ctx:
+        keep = ctx.enter_context(tc.tile_pool(name="keep", bufs=1))
+        grouped_pool = ctx.enter_context(tc.tile_pool(name="grouped", bufs=7))
+        acc_pool = ctx.enter_context(tc.psum_pool(name="acc", bufs=4))
+        tp_pool = ctx.enter_context(tc.psum_pool(name="tp", bufs=4))
+
+        ident = keep.tile([P, P], F32, name="ident")
+        masks.make_identity(nc, ident[:])
+        warm = keep.tile([P, 1], F32, name="warm")
+        nc.vector.memset(warm[:], 0.0)
+        nc.scalar.activation(out=warm[:], in_=warm[:], func=ACT.Square)
+
+        c_all = keep.tile([P, ND, J, W], F32, name="c_all")
+        r_all = keep.tile([P, ND, J, W], F32, name="r_all")
+        hn_sb = keep.tile([P, J, W], F32, name="hn_sb")
+        d_cz = keep.tile([P, 2, ND, J, W], BF16, name="d_cz")
+        d_cz_words = d_cz[:].bitcast(F32)
+        f_cz_codes = keep.tile([P, ND, J, 2 * P], U32, name="f_cz_codes", align_bytes=64)
+        f_cz_scales = keep.tile([P, ND, J, 2 * P], U8, name="f_cz_scales", align_bytes=64)
+        wih_codes = keep.tile([P, NG, W], U32, name="wih_codes", align_bytes=64)
+        wih_scales = keep.tile([P, NG, W], U8, name="wih_scales", align_bytes=64)
+        agg_codes = keep.tile([P, ND, W], U32, name="agg_codes", align_bytes=64)
+        agg_scales = keep.tile([P, ND, W], U8, name="agg_scales", align_bytes=64)
+
+        def copy_on(on_vector, out, in_):
+            if on_vector:
+                nc.vector.tensor_copy(out=out, in_=in_)
+            else:
+                nc.scalar.copy(out=out, in_=in_)
+
+        def interleave(on_vector, rows):
+            grouped = grouped_pool.tile([P, ROW], BF16, name="grouped", tag="grouped", align_bytes=64)
+            copy_on(on_vector, grouped[:].rearrange("p (w j) -> p w j", j=J), rows.rearrange("p j w -> p w j"))
+            return grouped
+
+        def quantize(x4, codes, scales, values):
+            nc.vector.quantize_mx(out=codes.bitcast(x4), scales=scales, in_=values)
+
+        def transpose_pairs(words_of):
+            bank = tp_pool.tile([P, W], F32, name="bank", tag="bank")
+            for k in range(2):
+                for u in range(2):
+                    nc.tensor.transpose(
+                        out=bank[:, (2 * k + u) * P : (2 * k + u + 1) * P],
+                        in_=words_of(k)[:, u : W // 2 : 2],
+                        identity=ident[:],
+                    )
+            return bank
+
+        def copy_pairs(on_vector, bank, turned):
+            copy_on(
+                on_vector,
+                turned.bitcast(F32).rearrange("q (k r u) -> q k r u", k=2, u=2),
+                bank[:].rearrange("q (k u r) -> q k r u", k=2, u=2),
+            )
+
+        with tc.tile_pool(name="stage1", bufs=1) as s1, tc.tile_pool(name="turned1", bufs=4) as turned1:
+            x_sb = s1.tile([P, J, W], BF16, name="x_sb")
+            g_sb = s1.tile([P, J, W], BF16, name="g_sb")
+            ds_sb = s1.tile([P, J, W], F32, name="ds_sb")
+            z_tiles = []
+            raw_tiles = []
+
+            def load_slot(j, split):
+                z_sb = s1.tile([P, ND, W], F32, name="z_sb", tag="z_sb", bufs=4)
+                z_tiles.append(z_sb)
+                nc.sync.dma_start(out=x_sb[:, j, :], in_=x_v[:, j, :])
+                for d0 in range(0, ND, split):
+                    d1 = d0 + split
+                    nc.sync.dma_start(out=c_all[:, d0:d1, j, :], in_=gates_v[:, d0:d1, j, GATE_C * W : (GATE_C + 1) * W])
+                    nc.sync.dma_start(out=z_sb[:, d0:d1, :], in_=gates_v[:, d0:d1, j, GATE_Z * W : (GATE_Z + 1) * W])
+                nc.sync.dma_start(out=g_sb[:, j, :], in_=g_v[:, j, :])
+                nc.sync.dma_start(out=ds_sb[:, j, :], in_=t_v[:, j, :])
+
+            def load_raw(rows):
+                raw = s1.tile([P, J, W], BF16, name="raw", tag="raw", bufs=6)
+                raw_tiles.append(raw)
+                nc.sync.dma_start(out=raw[:], in_=rows)
+
+            load_slot(0, 1)
+            load_slot(1, ND)
+            for g in range(NG):
+                load_raw(wih_v[g])
+            load_slot(2, ND)
+            for d in range(ND):
+                load_raw(agg_v[d])
+            load_slot(3, ND)
+            for d in range(ND):
+                nc.sync.dma_start(out=r_all[:, d, :, :], in_=gates_v[:, d, :, GATE_R * W : (GATE_R + 1) * W])
+            nc.sync.dma_start(out=hn_sb[:], in_=hn_v)
+
+            e_tiles = []
+            hsum_tiles = []
+
+            def new_slot():
+                e_tiles.append(s1.tile([P, ND, W], F32, name="e_sb", tag="e_sb", bufs=2))
+                hsum_tiles.append(acc_pool.tile([P, W], F32, name="hsum", tag="acc"))
+
+            def h_minus_c(j, d0, d1):
+                nc.vector.tensor_tensor(
+                    out=e_tiles[j][:, d0:d1, :],
+                    in0=x_sb[:, j : j + 1, :].to_broadcast([P, d1 - d0, W]),
+                    in1=c_all[:, d0:d1, j, :],
+                    op=ALU.subtract,
+                )
+
+            def times_z(j, d0, d1):
+                nc.vector.tensor_tensor(
+                    out=e_tiles[j][:, d0:d1, :], in0=z_tiles[j][:, d0:d1, :], in1=e_tiles[j][:, d0:d1, :], op=ALU.mult
+                )
+
+            def add_to_hsum(j, term, start, stop):
+                nc.tensor.matmul(out=hsum_tiles[j][:], lhsT=ident[:], rhs=term, start=start, stop=stop)
+
+            def square_c(j):
+                nc.scalar.activation(out=c_all[:, :, j, :], in_=c_all[:, :, j, :], func=ACT.Square)
+
+            def grad_times_t(j):
+                nc.vector.tensor_tensor(out=ds_sb[:, j, :], in0=g_sb[:, j, :], in1=ds_sb[:, j, :], op=ALU.mult)
+
+            new_slot()
+            h_minus_c(0, 0, 1)
+            add_to_hsum(0, c_all[:, 0, 0, :], True, False)
+            h_minus_c(0, 1, 2)
+            add_to_hsum(0, c_all[:, 1, 0, :], False, False)
+            times_z(0, 0, 1)
+            add_to_hsum(0, e_tiles[0][:, 0, :], False, False)
+            h_minus_c(0, 2, 3)
+            add_to_hsum(0, c_all[:, 2, 0, :], False, False)
+            times_z(0, 1, 2)
+            add_to_hsum(0, e_tiles[0][:, 1, :], False, False)
+            times_z(0, 2, 3)
+            add_to_hsum(0, e_tiles[0][:, 2, :], False, True)
+            square_c(0)
+            grad_times_t(0)
+
+            grouped_raw = {}
+            turned_tiles = {}
+            for j in range(J):
+                z_sb = z_tiles[j]
+                ds_b = ds_sb[:, j : j + 1, :].to_broadcast([P, ND, W])
+                nc.vector.scalar_tensor_tensor(
+                    out=ds_sb[:, j, :], in0=hsum_tiles[j][:], scalar=0.0, in1=ds_sb[:, j, :], op0=ALU.is_gt, op1=ALU.mult
+                )
+                if j + 1 < J:
+                    new_slot()
+                    h_minus_c(j + 1, 0, ND)
+                    for d in range(ND):
+                        add_to_hsum(j + 1, c_all[:, d, j + 1, :], d == 0, False)
+                nc.vector.scalar_tensor_tensor(
+                    out=z_sb[:], in0=z_sb[:], scalar=1.0, in1=ds_b, op0=ALU.subtract, op1=ALU.mult
+                )
+                if j + 1 < J:
+                    times_z(j + 1, 0, ND)
+                    for d in range(ND):
+                        add_to_hsum(j + 1, e_tiles[j + 1][:, d, :], False, d == ND - 1)
+                nc.vector.scalar_tensor_tensor(
+                    out=d_cz[:, 1, :, j, :], in0=e_tiles[j][:], scalar=-1.0, in1=z_sb[:], op0=ALU.mult, op1=ALU.mult
+                )
+                nc.vector.scalar_tensor_tensor(
+                    out=c_all[:, :, j, :], in0=c_all[:, :, j, :], scalar=1.0, in1=z_sb[:], op0=ALU.subtract, op1=ALU.mult
+                )
+                first = (0, 1, 3, 5)[j]
+                last = (1, 3, 5, 6)[j]
+                for i in range(first, last):
+                    grouped_raw[i] = interleave(False, raw_tiles[i][:])
+                    if i == first and j + 1 < J:
+                        square_c(j + 1)
+                if j == J - 1:
+                    nc.scalar.activation(out=r_all[:, 0, :, :], in_=r_all[:, 0, :, :], func=ACT.Square, bias=-0.5, scale=1.0)
+                nc.scalar.copy(out=d_cz[:, 0, :, j, :], in_=c_all[:, :, j, :])
+                if j + 1 < J:
+                    grad_times_t(j + 1)
+                if j > 0:
+                    for d in range(ND):
+                        quantize(E5M2X4, f_cz_codes[:, d, j - 1, :], f_cz_scales[:, d, j - 1, :], turned_tiles[(j - 1, d)][:])
+                for d in range(ND):
+                    bank = transpose_pairs(lambda k, d=d, j=j: d_cz_words[:, k, d, j, :])
+                    turned = turned1.tile([P, 2 * W], BF16, name="turned", tag="turned", align_bytes=64)
+                    turned_tiles[(j, d)] = turned
+                    copy_pairs(False, bank, turned[:])
+
+            nc.scalar.activation(out=r_all[:, 1, :, :], in_=r_all[:, 1, :, :], func=ACT.Square, bias=-0.5, scale=1.0)
+            nc.scalar.activation(out=r_all[:, 2, :, :], in_=r_all[:, 2, :, :], func=ACT.Square, bias=-0.5, scale=1.0)
+            for d in range(ND):
+                quantize(E5M2X4, f_cz_codes[:, d, J - 1, :], f_cz_scales[:, d, J - 1, :], turned_tiles[(J - 1, d)][:])
+            for i in range(NG):
+                quantize(E4M3X4, wih_codes[:, i, :], wih_scales[:, i, :], grouped_raw[i][:])
+            for i in range(ND):
+                quantize(E4M3X4, agg_codes[:, i, :], agg_scales[:, i, :], grouped_raw[NG + i][:])
+
+        with tc.tile_pool(name="stage2", bufs=1) as s2:
+            f_r_codes = s2.tile([P, ND, W], U32, name="f_r_codes", align_bytes=64)
+            f_r_scales = s2.tile([P, ND, W], U8, name="f_r_scales", align_bytes=64)
+            t_codes = s2.tile([P, NG, ND, W], U32, name="t_codes", align_bytes=64)
+            t_scales = s2.tile([P, NG, ND, W], U8, name="t_scales", align_bytes=64)
+            d_r_tiles = []
+
+            def store(on_vector, acc, rows):
+                result = s2.tile([P, W], F32, name="result", tag="result", bufs=6)
+                copy_on(on_vector, result[:], acc[:])
+                nc.sync.dma_start(out=rows, in_=result[:])
+
+            def grad_r(d):
+                nc.vector.scalar_tensor_tensor(
+                    out=r_all[:, d, :, :], in0=r_all[:, d, :, :], scalar=0.25, in1=c_all[:, d, :, :],
+                    op0=ALU.subtract, op1=ALU.mult,
+                )
+
+            def grad_r_times_hn(d):
+                d_r = s2.tile([P, J, W], BF16, name="d_r", tag="d_r", bufs=3)
+                d_r_tiles.append(d_r)
+                nc.vector.scalar_tensor_tensor(
+                    out=d_r[:], in0=r_all[:, d, :, :], scalar=-1.0, in1=hn_sb[:], op0=ALU.mult, op1=ALU.mult
+                )
+
+            def turn_r(d):
+                words = d_r_tiles[d][:].bitcast(F32)
+                turned = s2.tile([P, ROW], BF16, name="turned_r", tag="turned_r", bufs=2, align_bytes=64)
+                for half in range(2):
+                    bank = transpose_pairs(lambda k, half=half: words[:, 2 * half + k, :])
+                    copy_pairs(False, bank, turned[:, half * 2 * W : (half + 1) * 2 * W])
+                return turned
+
+            def product_0(d):
+                for j in range(J):
+                    acc = acc_pool.tile([P, W], F32, name="acc0", tag="acc")
+                    passes = (
+                        (f_cz_codes[:, d, j, 0:P], f_cz_scales[:, d, j, 0:P], GATE_C),
+                        (f_cz_codes[:, d, j, P : 2 * P], f_cz_scales[:, d, j, P : 2 * P], GATE_Z),
+                        (f_r_codes[:, d, j * P : (j + 1) * P], f_r_scales[:, d, j * P : (j + 1) * P], GATE_R),
+                    )
+                    for i, (codes, scales, g) in enumerate(passes):
+                        nc.tensor.matmul_mx(
+                            out=acc[:], lhsT=codes.bitcast(E5M2X4), lhsT_scale=scales,
+                            rhs=wih_codes[:, g, :].bitcast(E4M3X4), rhs_scale=wih_scales[:, g, :],
+                            start=(i == 0), stop=(i == NG - 1),
+                        )
+                    store(False, acc, out0_v[d][:, j, :])
+
+            def token_major(on_vector, g, d, rows):
+                grouped = interleave(on_vector, rows)
+                quantize(E5M2X4, t_codes[:, g, d, :], t_scales[:, g, d, :], grouped[:])
+
+            def product_1(g):
+                accs = []
+                for m in range(J):
+                    accs.append(acc_pool.tile([P, W], F32, name="acc1", tag="acc"))
+                for d in range(ND):
+                    for m in range(J):
+                        nc.tensor.matmul_mx(
+                            out=accs[m][:],
+                            lhsT=t_codes[:, g, d, m * P : (m + 1) * P].bitcast(E5M2X4),
+                            lhsT_scale=t_scales[:, g, d, m * P : (m + 1) * P],
+                            rhs=agg_codes[:, d, :].bitcast(E4M3X4), rhs_scale=agg_scales[:, d, :],
+                            start=(d == 0), stop=(d == ND - 1),
+                        )
+                for m in range(J):
+                    store(g == GATE_R and m % 2 == 1, accs[m], out1_v[g * J + m])
+
+            grad_r(0)
+            grad_r_times_hn(0)
+            turned_0 = turn_r(0)
+            grad_r(1)
+            quantize(E5M2X4, f_r_codes[:, 0, :], f_r_scales[:, 0, :], turned_0[:])
+            grad_r_times_hn(1)
+            product_0(0)
+            turned_1 = turn_r(1)
+            token_major(False, GATE_C, 0, d_cz[:, 0, 0, :, :])
+            grad_r(2)
+            quantize(E5M2X4, f_r_codes[:, 1, :], f_r_scales[:, 1, :], turned_1[:])
+            grad_r_times_hn(2)
+            product_0(1)
+            turned_2 = turn_r(2)
+            token_major(False, GATE_C, 1, d_cz[:, 0, 1, :, :])
+            token_major(False, GATE_C, 2, d_cz[:, 0, 2, :, :])
+            quantize(E5M2X4, f_r_codes[:, 2, :], f_r_scales[:, 2, :], turned_2[:])
+            product_0(2)
+            product_1(GATE_C)
+            token_major(False, GATE_Z, 0, d_cz[:, 1, 0, :, :])
+            token_major(False, GATE_Z, 1, d_cz[:, 1, 1, :, :])
+            token_major(True, GATE_Z, 2, d_cz[:, 1, 2, :, :])
+            product_1(GATE_Z)
+            for d in range(ND):
+                token_major(True, GATE_R, d, d_r_tiles[d][:])
+            product_1(GATE_R)

@@ -71,7 +71,11 @@ def tile_graphconvolution_pb_v_kernel(
 
         def interleave(on_vector, rows):
             grouped = grouped_pool.tile([P, ROW], BF16, name="grouped", tag="grouped", align_bytes=64)
-            copy_on(on_vector, grouped[:].rearrange("p (w j) -> p w j", j=J), rows.rearrange("p j w -> p w j"))
+            copy_on(
+                on_vector,
+                grouped[:].rearrange("p (c i j) -> p c j i", i=4, j=J),
+                rows.rearrange("p j (c i) -> p c j i", i=4),
+            )
             return grouped
 
         def quantize(x4, codes, scales, values):

@@ -19,6 +19,12 @@ ND = 3
 NG = 3
 ROW = J * W
 GATE_R, GATE_Z, GATE_C = 0, 1, 2
+RAW_BUFS = 4
+QRAW = ((), (0, 1, 2), (3, 4))
+SPARE_A = (1, 0, 0)
+SPARE_B = (0, 1, 1)
+SPARE_C = (1, 1, 0)
+SPARE_D = (0, 1, 0)
 
 FLOPS = 2 * 2 * (ND * W) * (NG * W) * W
 BYTES = 2 * (ND * W * W + W * W + NG * W * W + W * W) + 4 * (ND * W * NG * W + 2 * W * W) + 4 * 2 * ND * W * W
@@ -41,9 +47,12 @@ def tile_graphconvolution_pb_v_kernel(
 
     with ExitStack() as ctx:
         keep = ctx.enter_context(tc.tile_pool(name="keep", bufs=1))
-        grouped_pool = ctx.enter_context(tc.tile_pool(name="grouped", bufs=7))
+        grouped_pool = ctx.enter_context(tc.tile_pool(name="grouped", bufs=4))
+        turned_pool = ctx.enter_context(tc.tile_pool(name="turned", bufs=6))
+        result_pool = ctx.enter_context(tc.tile_pool(name="result", bufs=6))
         acc_pool = ctx.enter_context(tc.psum_pool(name="acc", bufs=4))
         tp_pool = ctx.enter_context(tc.psum_pool(name="tp", bufs=4))
+        ctx.enter_context(tc.manual_schedule())
 
         ident = keep.tile([P, P], F32, name="ident")
         masks.make_identity(nc, ident[:])
@@ -51,13 +60,8 @@ def tile_graphconvolution_pb_v_kernel(
         nc.vector.memset(warm[:], 0.0)
         nc.scalar.activation(out=warm[:], in_=warm[:], func=ACT.Square)
 
-        c_all = keep.tile([P, ND, J, W], F32, name="c_all")
-        r_all = keep.tile([P, ND, J, W], F32, name="r_all")
-        hn_sb = keep.tile([P, J, W], F32, name="hn_sb")
-        d_cz = keep.tile([P, 2, ND, J, W], BF16, name="d_cz")
-        d_cz_words = d_cz[:].bitcast(F32)
-        f_cz_codes = keep.tile([P, ND, J, 2 * P], U32, name="f_cz_codes", align_bytes=64)
-        f_cz_scales = keep.tile([P, ND, J, 2 * P], U8, name="f_cz_scales", align_bytes=64)
+        d_all = keep.tile([P, NG, ND, J, W], BF16, name="d_all")
+        d_words = d_all[:].bitcast(F32)
         wih_codes = keep.tile([P, NG, W], U32, name="wih_codes", align_bytes=64)
         wih_scales = keep.tile([P, NG, W], U8, name="wih_scales", align_bytes=64)
         agg_codes = keep.tile([P, ND, W], U32, name="agg_codes", align_bytes=64)
@@ -81,71 +85,111 @@ def tile_graphconvolution_pb_v_kernel(
         def quantize(x4, codes, scales, values):
             nc.vector.quantize_mx(out=codes.bitcast(x4), scales=scales, in_=values)
 
-        def transpose_pairs(words_of):
+        def transpose_pairs(views):
             bank = tp_pool.tile([P, W], F32, name="bank", tag="bank")
-            for k in range(2):
+            for k, words in enumerate(views):
                 for u in range(2):
                     nc.tensor.transpose(
-                        out=bank[:, (2 * k + u) * P : (2 * k + u + 1) * P],
-                        in_=words_of(k)[:, u : W // 2 : 2],
-                        identity=ident[:],
+                        out=bank[:, (2 * k + u) * P : (2 * k + u + 1) * P], in_=words[:, u : W // 2 : 2], identity=ident[:]
                     )
             return bank
 
-        def copy_pairs(on_vector, bank, turned):
+        def copy_pairs(on_vector, bank, n):
+            turned = turned_pool.tile([P, 2 * W], BF16, name="turned", tag="turned", align_bytes=64)
             copy_on(
                 on_vector,
-                turned.bitcast(F32).rearrange("q (k r u) -> q k r u", k=2, u=2),
-                bank[:].rearrange("q (k u r) -> q k r u", k=2, u=2),
+                turned[:, 0 : n * W].bitcast(F32).rearrange("q (k r u) -> q k r u", k=n, u=2),
+                bank[:, 0 : n * 2 * P].rearrange("q (k u r) -> q k r u", k=n, u=2),
             )
+            return turned
 
-        with tc.tile_pool(name="stage1", bufs=1) as s1, tc.tile_pool(name="turned1", bufs=4) as turned1:
+        def store(on_vector, acc, rows):
+            result = result_pool.tile([P, W], F32, name="result", tag="result")
+            copy_on(on_vector, result[:], acc[:])
+            nc.sync.dma_start(out=rows, in_=result[:])
+
+        grouped_raw = {}
+        raw_tiles = []
+
+        def interleave_raw(on_vector, i):
+            grouped_raw[i] = interleave(on_vector, raw_tiles[i][:])
+
+        def quantize_raw(i):
+            if i < NG:
+                quantize(E4M3X4, wih_codes[:, i, :], wih_scales[:, i, :], grouped_raw[i][:])
+            else:
+                quantize(E4M3X4, agg_codes[:, i - NG, :], agg_scales[:, i - NG, :], grouped_raw[i][:])
+
+        with tc.tile_pool(name="stage1", bufs=1) as s1:
             x_sb = s1.tile([P, J, W], BF16, name="x_sb")
             g_sb = s1.tile([P, J, W], BF16, name="g_sb")
             ds_sb = s1.tile([P, J, W], F32, name="ds_sb")
-            z_tiles = []
-            raw_tiles = []
+            hn_sb = s1.tile([P, J, W], F32, name="hn_sb")
+            c_tiles, z_tiles, r_tiles, e_tiles, hsum_tiles, f_codes, f_scales = {}, {}, {}, {}, {}, {}, {}
+            banks, turned = {}, {}
+            accs = {}
 
-            def load_slot(j, split):
-                z_sb = s1.tile([P, ND, W], F32, name="z_sb", tag="z_sb", bufs=4)
-                z_tiles.append(z_sb)
+            def load_gate(out, j, d0, d1, g):
+                nc.sync.dma_start(out=out, in_=gates_v[:, d0:d1, j, g * W : (g + 1) * W])
+
+            def alloc_slot(j):
+                c_tiles[j] = s1.tile([P, ND, W], F32, name="c_sb", tag="c_sb", bufs=3)
+                z_tiles[j] = s1.tile([P, ND, W], F32, name="z_sb", tag="z_sb", bufs=3)
+                r_tiles[j] = s1.tile([P, ND, W], F32, name="r_sb", tag="r_sb", bufs=3)
+
+            def load_x_c(j):
                 nc.sync.dma_start(out=x_sb[:, j, :], in_=x_v[:, j, :])
-                for d0 in range(0, ND, split):
-                    d1 = d0 + split
-                    nc.sync.dma_start(out=c_all[:, d0:d1, j, :], in_=gates_v[:, d0:d1, j, GATE_C * W : (GATE_C + 1) * W])
-                    nc.sync.dma_start(out=z_sb[:, d0:d1, :], in_=gates_v[:, d0:d1, j, GATE_Z * W : (GATE_Z + 1) * W])
+                load_gate(c_tiles[j][:], j, 0, ND, GATE_C)
+
+            def load_g_t(j):
                 nc.sync.dma_start(out=g_sb[:, j, :], in_=g_v[:, j, :])
                 nc.sync.dma_start(out=ds_sb[:, j, :], in_=t_v[:, j, :])
 
-            def load_raw(rows):
-                raw = s1.tile([P, J, W], BF16, name="raw", tag="raw", bufs=6)
-                raw_tiles.append(raw)
-                nc.sync.dma_start(out=raw[:], in_=rows)
+            def load_r_hn(j):
+                load_gate(r_tiles[j][:], j, 0, ND, GATE_R)
+                nc.sync.dma_start(out=hn_sb[:, j, :], in_=hn_v[:, j, :])
 
-            load_slot(0, 1)
-            load_slot(1, ND)
-            for g in range(NG):
-                load_raw(wih_v[g])
-            load_slot(2, ND)
+            def load_raw(i):
+                raw_tiles.append(s1.tile([P, J, W], BF16, name="raw", tag="raw", bufs=RAW_BUFS))
+                nc.sync.dma_start(out=raw_tiles[i][:], in_=wih_v[i] if i < NG else agg_v[i - NG])
+
+            def load_slot(j):
+                alloc_slot(j)
+                load_x_c(j)
+                load_gate(z_tiles[j][:], j, 0, ND, GATE_Z)
+                load_g_t(j)
+                load_r_hn(j)
+
+            alloc_slot(0)
+            nc.sync.dma_start(out=x_sb[:, 0, :], in_=x_v[:, 0, :])
             for d in range(ND):
-                load_raw(agg_v[d])
-            load_slot(3, ND)
-            for d in range(ND):
-                nc.sync.dma_start(out=r_all[:, d, :, :], in_=gates_v[:, d, :, GATE_R * W : (GATE_R + 1) * W])
-            nc.sync.dma_start(out=hn_sb[:], in_=hn_v)
+                load_gate(c_tiles[0][:, d : d + 1, :], 0, d, d + 1, GATE_C)
+                load_gate(z_tiles[0][:, d : d + 1, :], 0, d, d + 1, GATE_Z)
+            alloc_slot(1)
+            load_x_c(1)
+            load_g_t(0)
+            load_gate(z_tiles[1][:], 1, 0, ND, GATE_Z)
+            load_raw(0)
+            load_r_hn(0)
+            alloc_slot(2)
+            load_x_c(2)
+            load_raw(1)
+            load_g_t(1)
+            load_gate(z_tiles[2][:], 2, 0, ND, GATE_Z)
+            load_raw(2)
+            load_r_hn(1)
+            load_g_t(2)
+            load_r_hn(2)
+            load_raw(3)
 
-            e_tiles = []
-            hsum_tiles = []
-
-            def new_slot():
-                e_tiles.append(s1.tile([P, ND, W], F32, name="e_sb", tag="e_sb", bufs=2))
-                hsum_tiles.append(acc_pool.tile([P, W], F32, name="hsum", tag="acc"))
+            def new_slot(j):
+                e_tiles[j] = s1.tile([P, ND, W], F32, name="e_sb", tag="e_sb", bufs=2)
 
             def h_minus_c(j, d0, d1):
                 nc.vector.tensor_tensor(
                     out=e_tiles[j][:, d0:d1, :],
                     in0=x_sb[:, j : j + 1, :].to_broadcast([P, d1 - d0, W]),
-                    in1=c_all[:, d0:d1, j, :],
+                    in1=c_tiles[j][:, d0:d1, :],
                     op=ALU.subtract,
                 )
 
@@ -157,175 +201,295 @@ def tile_graphconvolution_pb_v_kernel(
             def add_to_hsum(j, term, start, stop):
                 nc.tensor.matmul(out=hsum_tiles[j][:], lhsT=ident[:], rhs=term, start=start, stop=stop)
 
+            def add_c(j):
+                hsum_tiles[j] = acc_pool.tile([P, W], F32, name="hsum", tag="acc")
+                for d in range(ND):
+                    add_to_hsum(j, c_tiles[j][:, d, :], d == 0, False)
+
+            def add_ze(j):
+                for d in range(ND):
+                    add_to_hsum(j, e_tiles[j][:, d, :], False, d == ND - 1)
+
             def square_c(j):
-                nc.scalar.activation(out=c_all[:, :, j, :], in_=c_all[:, :, j, :], func=ACT.Square)
+                nc.scalar.activation(out=c_tiles[j][:], in_=c_tiles[j][:], func=ACT.Square)
+
+            def square_r(j):
+                nc.scalar.activation(out=r_tiles[j][:], in_=r_tiles[j][:], func=ACT.Square, bias=-0.5, scale=1.0)
 
             def grad_times_t(j):
                 nc.vector.tensor_tensor(out=ds_sb[:, j, :], in0=g_sb[:, j, :], in1=ds_sb[:, j, :], op=ALU.mult)
 
-            new_slot()
+            def mask(j):
+                nc.vector.scalar_tensor_tensor(
+                    out=ds_sb[:, j, :], in0=hsum_tiles[j][:], scalar=0.0, in1=ds_sb[:, j, :], op0=ALU.is_gt, op1=ALU.mult
+                )
+
+            def a_op(j):
+                nc.vector.scalar_tensor_tensor(
+                    out=z_tiles[j][:], in0=z_tiles[j][:], scalar=1.0, in1=ds_sb[:, j : j + 1, :].to_broadcast([P, ND, W]),
+                    op0=ALU.subtract, op1=ALU.mult,
+                )
+
+            def dz_op(j):
+                nc.vector.scalar_tensor_tensor(
+                    out=d_all[:, 1, :, j, :], in0=e_tiles[j][:], scalar=-1.0, in1=z_tiles[j][:], op0=ALU.mult, op1=ALU.mult
+                )
+
+            def dc_op(j):
+                nc.vector.scalar_tensor_tensor(
+                    out=c_tiles[j][:], in0=c_tiles[j][:], scalar=1.0, in1=z_tiles[j][:], op0=ALU.subtract, op1=ALU.mult
+                )
+
+            def cast_dc(j):
+                nc.scalar.copy(out=d_all[:, 0, :, j, :], in_=c_tiles[j][:])
+
+            def b_op(j):
+                nc.vector.scalar_tensor_tensor(
+                    out=r_tiles[j][:], in0=r_tiles[j][:], scalar=0.25, in1=c_tiles[j][:], op0=ALU.subtract, op1=ALU.mult
+                )
+
+            def dr_op(j):
+                nc.vector.scalar_tensor_tensor(
+                    out=d_all[:, 2, :, j, :], in0=r_tiles[j][:], scalar=-1.0,
+                    in1=hn_sb[:, j : j + 1, :].to_broadcast([P, ND, W]), op0=ALU.mult, op1=ALU.mult,
+                )
+
+            def turn_cz(j):
+                for d in range(ND):
+                    banks[(j, d)] = transpose_pairs([d_words[:, 0, d, j, :], d_words[:, 1, d, j, :]])
+
+            def turn_r(j):
+                banks[(j, 3)] = transpose_pairs([d_words[:, 2, 0, j, :], d_words[:, 2, 1, j, :]])
+                banks[(j, 4)] = transpose_pairs([d_words[:, 2, 2, j, :]])
+
+            def copy_turned(on_vector, j, i):
+                turned[(j, i)] = copy_pairs(on_vector, banks[(j, i)], 1 if i == 4 else 2)
+
+            def quantize_turned(j, i):
+                if i == 0:
+                    f_codes[j] = s1.tile([P, 9 * P], U32, name="f_codes", tag="f_codes", bufs=2, align_bytes=64)
+                    f_scales[j] = s1.tile([P, 9 * P], U8, name="f_scales", tag="f_scales", bufs=2, align_bytes=64)
+                n = 1 if i == 4 else 2
+                quantize(
+                    E5M2X4, f_codes[j][:, i * 2 * P : (i * 2 + n) * P], f_scales[j][:, i * 2 * P : (i * 2 + n) * P],
+                    turned[(j, i)][:, 0 : n * W],
+                )
+
+            def mm0(d, j):
+                acc = acc_pool.tile([P, W], F32, name="acc0", tag="acc")
+                accs[(d, j)] = acc
+                for i, (col, g) in enumerate(((2 * d, GATE_C), (2 * d + 1, GATE_Z), (6 + d, GATE_R))):
+                    nc.tensor.matmul_mx(
+                        out=acc[:], lhsT=f_codes[j][:, col * P : (col + 1) * P].bitcast(E5M2X4),
+                        lhsT_scale=f_scales[j][:, col * P : (col + 1) * P],
+                        rhs=wih_codes[:, g, :].bitcast(E4M3X4), rhs_scale=wih_scales[:, g, :],
+                        start=(i == 0), stop=(i == NG - 1),
+                    )
+
+            def out0(on_vector, d, j):
+                store(on_vector, accs[(d, j)], out0_v[d][:, j, :])
+
+            new_slot(0)
+            hsum_tiles[0] = acc_pool.tile([P, W], F32, name="hsum", tag="acc")
             h_minus_c(0, 0, 1)
-            add_to_hsum(0, c_all[:, 0, 0, :], True, False)
+            add_to_hsum(0, c_tiles[0][:, 0, :], True, False)
             h_minus_c(0, 1, 2)
-            add_to_hsum(0, c_all[:, 1, 0, :], False, False)
+            add_to_hsum(0, c_tiles[0][:, 1, :], False, False)
             times_z(0, 0, 1)
             add_to_hsum(0, e_tiles[0][:, 0, :], False, False)
             h_minus_c(0, 2, 3)
-            add_to_hsum(0, c_all[:, 2, 0, :], False, False)
+            add_to_hsum(0, c_tiles[0][:, 2, :], False, False)
             times_z(0, 1, 2)
             add_to_hsum(0, e_tiles[0][:, 1, :], False, False)
             times_z(0, 2, 3)
             add_to_hsum(0, e_tiles[0][:, 2, :], False, True)
+            new_slot(1)
+            h_minus_c(1, 0, ND)
             square_c(0)
             grad_times_t(0)
 
-            grouped_raw = {}
-            turned_tiles = {}
-            for j in range(J):
-                z_sb = z_tiles[j]
-                ds_b = ds_sb[:, j : j + 1, :].to_broadcast([P, ND, W])
-                nc.vector.scalar_tensor_tensor(
-                    out=ds_sb[:, j, :], in0=hsum_tiles[j][:], scalar=0.0, in1=ds_sb[:, j, :], op0=ALU.is_gt, op1=ALU.mult
+            t_codes = keep.tile([P, NG, ND, W], U32, name="t_codes", align_bytes=64)
+            t_scales = keep.tile([P, NG, ND, W], U8, name="t_scales", align_bytes=64)
+            grouped_t = {}
+            accs1 = {}
+
+            def group_t(on_vector, g, d):
+                grouped_t[(g, d)] = interleave(on_vector, d_all[:, 2 - g, d, :, :])
+
+            def group_part(g, d, m):
+                if m == 0:
+                    grouped_t[(g, d)] = grouped_pool.tile([P, ROW], BF16, name="grouped", tag="grouped", align_bytes=64)
+                nc.vector.tensor_copy(
+                    out=grouped_t[(g, d)][:, m * J * P : (m + 1) * J * P].rearrange("p (c i j) -> p c j i", i=4, j=J),
+                    in_=d_all[:, 2 - g, d, :, m * P : (m + 1) * P].rearrange("p j (c i) -> p c j i", i=4),
                 )
+
+            def quantize_part(g, d, m):
+                quantize(
+                    E5M2X4, t_codes[:, g, d, m * P : (m + 1) * P], t_scales[:, g, d, m * P : (m + 1) * P],
+                    grouped_t[(g, d)][:, m * J * P : (m + 1) * J * P],
+                )
+
+            def quantize_t(g, d):
+                quantize(E5M2X4, t_codes[:, g, d, :], t_scales[:, g, d, :], grouped_t[(g, d)][:])
+
+            def mm1(g, m, d0, d1):
+                if d0 == 0 and g == GATE_C:
+                    accs1[(g, m)] = acc_pool.tile([P, W], F32, name="acc1", tag="acc")
+                elif d0 == 0:
+                    accs1[(g, m)] = tp_pool.tile([P, W], F32, name="bank", tag="bank")
+                for d in range(d0, d1):
+                    nc.tensor.matmul_mx(
+                        out=accs1[(g, m)][:],
+                        lhsT=t_codes[:, g, d, m * P : (m + 1) * P].bitcast(E5M2X4),
+                        lhsT_scale=t_scales[:, g, d, m * P : (m + 1) * P],
+                        rhs=agg_codes[:, d, :].bitcast(E4M3X4), rhs_scale=agg_scales[:, d, :],
+                        start=(d == 0), stop=(d == ND - 1),
+                    )
+
+            def out1(on_vector, g, m):
+                store(on_vector, accs1[(g, m)], out1_v[g * J + m])
+
+
+            spare = [lambda i=i: interleave_raw(False, i) for i in range(NG + ND)]
+            for j in range(J - 1):
+                mask(j)
                 if j + 1 < J:
-                    new_slot()
-                    h_minus_c(j + 1, 0, ND)
-                    for d in range(ND):
-                        add_to_hsum(j + 1, c_all[:, d, j + 1, :], d == 0, False)
-                nc.vector.scalar_tensor_tensor(
-                    out=z_sb[:], in0=z_sb[:], scalar=1.0, in1=ds_b, op0=ALU.subtract, op1=ALU.mult
-                )
+                    add_c(j + 1)
+                if j > 0:
+                    copy_turned(False, j - 1, 3)
+                    copy_turned(False, j - 1, 4)
+                    quantize_turned(j - 1, 0)
+                a_op(j)
+                if j > 0:
+                    quantize_turned(j - 1, 1)
                 if j + 1 < J:
                     times_z(j + 1, 0, ND)
+                    add_ze(j + 1)
+                if j > 0:
+                    quantize_turned(j - 1, 2)
+                if j + 1 < J:
+                    dz_op(j)
+                else:
+                    dc_op(j)
+                if j > 0:
+                    quantize_turned(j - 1, 3)
+                if j + 1 < J:
+                    dc_op(j)
+                else:
+                    dz_op(j)
+                if j > 0:
+                    quantize_turned(j - 1, 4)
+                if j > 1:
                     for d in range(ND):
-                        add_to_hsum(j + 1, e_tiles[j + 1][:, d, :], False, d == ND - 1)
-                nc.vector.scalar_tensor_tensor(
-                    out=d_cz[:, 1, :, j, :], in0=e_tiles[j][:], scalar=-1.0, in1=z_sb[:], op0=ALU.mult, op1=ALU.mult
-                )
-                nc.vector.scalar_tensor_tensor(
-                    out=c_all[:, :, j, :], in0=c_all[:, :, j, :], scalar=1.0, in1=z_sb[:], op0=ALU.subtract, op1=ALU.mult
-                )
-                first = (0, 1, 3, 5)[j]
-                last = (1, 3, 5, 6)[j]
-                for i in range(first, last):
-                    grouped_raw[i] = interleave(False, raw_tiles[i][:])
-                    if i == first and j + 1 < J:
-                        square_c(j + 1)
-                if j == J - 1:
-                    nc.scalar.activation(out=r_all[:, 0, :, :], in_=r_all[:, 0, :, :], func=ACT.Square, bias=-0.5, scale=1.0)
-                nc.scalar.copy(out=d_cz[:, 0, :, j, :], in_=c_all[:, :, j, :])
+                        mm0(d, j - 1)
+                for i in range(SPARE_A[j]):
+                    spare.pop(0)()
+                square_r(j)
+                if j + 1 < J:
+                    square_c(j + 1)
+                for i in range(SPARE_B[j]):
+                    spare.pop(0)()
+                cast_dc(j)
+                turn_cz(j)
+                if j + 2 < J:
+                    new_slot(j + 2)
+                    h_minus_c(j + 2, 0, ND)
+                b_op(j)
                 if j + 1 < J:
                     grad_times_t(j + 1)
-                if j > 0:
+                dr_op(j)
+                for i in range(SPARE_C[j]):
+                    spare.pop(0)()
+                if j > 1:
                     for d in range(ND):
-                        quantize(E5M2X4, f_cz_codes[:, d, j - 1, :], f_cz_scales[:, d, j - 1, :], turned_tiles[(j - 1, d)][:])
-                for d in range(ND):
-                    bank = transpose_pairs(lambda k, d=d, j=j: d_cz_words[:, k, d, j, :])
-                    turned = turned1.tile([P, 2 * W], BF16, name="turned", tag="turned", align_bytes=64)
-                    turned_tiles[(j, d)] = turned
-                    copy_pairs(False, bank, turned[:])
+                        out0(False, d, j - 1)
+                for i in range(3):
+                    copy_turned(False, j, i)
+                turn_r(j)
+                for i in QRAW[j]:
+                    quantize_raw(i)
+                for i in range(SPARE_D[j]):
+                    spare.pop(0)()
+                if j == 1:
+                    for d in range(ND):
+                        mm0(d, 0)
+                    for d in range(ND):
+                        out0(False, d, 0)
+                if j == 0:
+                    load_raw(4)
+                    load_raw(5)
+                    load_slot(3)
 
-            nc.scalar.activation(out=r_all[:, 1, :, :], in_=r_all[:, 1, :, :], func=ACT.Square, bias=-0.5, scale=1.0)
-            nc.scalar.activation(out=r_all[:, 2, :, :], in_=r_all[:, 2, :, :], func=ACT.Square, bias=-0.5, scale=1.0)
+
+            L = J - 1
+            mask(L)
+            copy_turned(False, L - 1, 3)
+            copy_turned(False, L - 1, 4)
+            quantize_turned(L - 1, 0)
+            a_op(L)
+            quantize_turned(L - 1, 1)
+            dc_op(L)
+            square_r(L)
+            cast_dc(L)
+            quantize_turned(L - 1, 2)
+            dz_op(L)
+            quantize_turned(L - 1, 3)
+            quantize_turned(L - 1, 4)
             for d in range(ND):
-                quantize(E5M2X4, f_cz_codes[:, d, J - 1, :], f_cz_scales[:, d, J - 1, :], turned_tiles[(J - 1, d)][:])
-            for i in range(NG):
-                quantize(E4M3X4, wih_codes[:, i, :], wih_scales[:, i, :], grouped_raw[i][:])
-            for i in range(ND):
-                quantize(E4M3X4, agg_codes[:, i, :], agg_scales[:, i, :], grouped_raw[NG + i][:])
-
-        with tc.tile_pool(name="stage2", bufs=1) as s2:
-            f_r_codes = s2.tile([P, ND, W], U32, name="f_r_codes", align_bytes=64)
-            f_r_scales = s2.tile([P, ND, W], U8, name="f_r_scales", align_bytes=64)
-            t_codes = s2.tile([P, NG, ND, W], U32, name="t_codes", align_bytes=64)
-            t_scales = s2.tile([P, NG, ND, W], U8, name="t_scales", align_bytes=64)
-            d_r_tiles = []
-
-            def store(on_vector, acc, rows):
-                result = s2.tile([P, W], F32, name="result", tag="result", bufs=6)
-                copy_on(on_vector, result[:], acc[:])
-                nc.sync.dma_start(out=rows, in_=result[:])
-
-            def grad_r(d):
-                nc.vector.scalar_tensor_tensor(
-                    out=r_all[:, d, :, :], in0=r_all[:, d, :, :], scalar=0.25, in1=c_all[:, d, :, :],
-                    op0=ALU.subtract, op1=ALU.mult,
-                )
-
-            def grad_r_times_hn(d):
-                d_r = s2.tile([P, J, W], BF16, name="d_r", tag="d_r", bufs=3)
-                d_r_tiles.append(d_r)
-                nc.vector.scalar_tensor_tensor(
-                    out=d_r[:], in0=r_all[:, d, :, :], scalar=-1.0, in1=hn_sb[:], op0=ALU.mult, op1=ALU.mult
-                )
-
-            def turn_r(d):
-                words = d_r_tiles[d][:].bitcast(F32)
-                turned = s2.tile([P, ROW], BF16, name="turned_r", tag="turned_r", bufs=2, align_bytes=64)
-                for half in range(2):
-                    bank = transpose_pairs(lambda k, half=half: words[:, 2 * half + k, :])
-                    copy_pairs(False, bank, turned[:, half * 2 * W : (half + 1) * 2 * W])
-                return turned
-
-            def product_0(d):
-                for j in range(J):
-                    acc = acc_pool.tile([P, W], F32, name="acc0", tag="acc")
-                    passes = (
-                        (f_cz_codes[:, d, j, 0:P], f_cz_scales[:, d, j, 0:P], GATE_C),
-                        (f_cz_codes[:, d, j, P : 2 * P], f_cz_scales[:, d, j, P : 2 * P], GATE_Z),
-                        (f_r_codes[:, d, j * P : (j + 1) * P], f_r_scales[:, d, j * P : (j + 1) * P], GATE_R),
-                    )
-                    for i, (codes, scales, g) in enumerate(passes):
-                        nc.tensor.matmul_mx(
-                            out=acc[:], lhsT=codes.bitcast(E5M2X4), lhsT_scale=scales,
-                            rhs=wih_codes[:, g, :].bitcast(E4M3X4), rhs_scale=wih_scales[:, g, :],
-                            start=(i == 0), stop=(i == NG - 1),
-                        )
-                    store(False, acc, out0_v[d][:, j, :])
-
-            def token_major(on_vector, g, d, rows):
-                grouped = interleave(on_vector, rows)
-                quantize(E5M2X4, t_codes[:, g, d, :], t_scales[:, g, d, :], grouped[:])
-
-            def product_1(g):
-                accs = []
-                for m in range(J):
-                    accs.append(acc_pool.tile([P, W], F32, name="acc1", tag="acc"))
-                for d in range(ND):
-                    for m in range(J):
-                        nc.tensor.matmul_mx(
-                            out=accs[m][:],
-                            lhsT=t_codes[:, g, d, m * P : (m + 1) * P].bitcast(E5M2X4),
-                            lhsT_scale=t_scales[:, g, d, m * P : (m + 1) * P],
-                            rhs=agg_codes[:, d, :].bitcast(E4M3X4), rhs_scale=agg_scales[:, d, :],
-                            start=(d == 0), stop=(d == ND - 1),
-                        )
-                for m in range(J):
-                    store(g == GATE_R and m % 2 == 1, accs[m], out1_v[g * J + m])
-
-            grad_r(0)
-            grad_r_times_hn(0)
-            turned_0 = turn_r(0)
-            grad_r(1)
-            quantize(E5M2X4, f_r_codes[:, 0, :], f_r_scales[:, 0, :], turned_0[:])
-            grad_r_times_hn(1)
-            product_0(0)
-            turned_1 = turn_r(1)
-            token_major(False, GATE_C, 0, d_cz[:, 0, 0, :, :])
-            grad_r(2)
-            quantize(E5M2X4, f_r_codes[:, 1, :], f_r_scales[:, 1, :], turned_1[:])
-            grad_r_times_hn(2)
-            product_0(1)
-            turned_2 = turn_r(2)
-            token_major(False, GATE_C, 1, d_cz[:, 0, 1, :, :])
-            token_major(False, GATE_C, 2, d_cz[:, 0, 2, :, :])
-            quantize(E5M2X4, f_r_codes[:, 2, :], f_r_scales[:, 2, :], turned_2[:])
-            product_0(2)
-            product_1(GATE_C)
-            token_major(False, GATE_Z, 0, d_cz[:, 1, 0, :, :])
-            token_major(False, GATE_Z, 1, d_cz[:, 1, 1, :, :])
-            token_major(True, GATE_Z, 2, d_cz[:, 1, 2, :, :])
-            product_1(GATE_Z)
+                mm0(d, L - 1)
+            turn_cz(L)
+            b_op(L)
+            group_t(False, GATE_C, 0)
+            quantize_raw(5)
+            dr_op(L)
             for d in range(ND):
-                token_major(True, GATE_R, d, d_r_tiles[d][:])
-            product_1(GATE_R)
+                out0(False, d, L - 1)
+            for i in range(3):
+                copy_turned(False, L, i)
+            turn_r(L)
+            copy_turned(False, L, 3)
+            copy_turned(False, L, 4)
+            group_t(True, GATE_Z, 0)
+            group_t(True, GATE_Z, 1)
+            for i in range(5):
+                quantize_turned(L, i)
+            for d in range(ND):
+                mm0(d, L)
+            quantize_t(GATE_C, 0)
+            group_t(False, GATE_C, 1)
+            quantize_t(GATE_Z, 0)
+            group_t(True, GATE_Z, 2)
+            quantize_t(GATE_Z, 1)
+            quantize_t(GATE_Z, 2)
+            for d in range(ND):
+                for m in range(J):
+                    mm1(GATE_Z, m, d, d + 1)
+            group_t(False, GATE_C, 2)
+            quantize_t(GATE_C, 1)
+            group_t(True, GATE_R, 0)
+            quantize_t(GATE_C, 2)
+            for d in range(ND):
+                out0(False, d, L)
+            for m in range(J):
+                mm1(GATE_C, m, 0, ND)
+            for m in range(J):
+                out1(False, GATE_Z, m)
+            group_t(True, GATE_R, 1)
+            quantize_t(GATE_R, 0)
+            for m in range(J):
+                mm1(GATE_R, m, 0, 1)
+            group_part(GATE_R, 2, 0)
+            quantize_t(GATE_R, 1)
+            for m in range(J):
+                mm1(GATE_R, m, 1, 2)
+            for m in range(J):
+                out1(False, GATE_C, m)
+            group_part(GATE_R, 2, 1)
+            for m in range(J):
+                quantize_part(GATE_R, 2, m)
+                if m + 2 < J:
+                    group_part(GATE_R, 2, m + 2)
+                mm1(GATE_R, m, 2, 3)
+            for m in range(J):
+                out1(m % 2 == 1, GATE_R, m)

@@ -19,12 +19,12 @@ ND = 3
 NG = 3
 ROW = J * W
 GATE_R, GATE_Z, GATE_C = 0, 1, 2
-RAW_BUFS = 4
-QRAW = ((), (0, 1, 2), (3, 4))
+DC, DZ, DR = 0, 1, 2
+LAST = J - 1
 SPARE_A = (1, 0, 0)
 SPARE_B = (0, 1, 1)
 SPARE_C = (1, 1, 0)
-SPARE_D = (0, 1, 0)
+RUN = 8
 
 FLOPS = 2 * 2 * (ND * W) * (NG * W) * W
 BYTES = 2 * (ND * W * W + W * W + NG * W * W + W * W) + 4 * (ND * W * NG * W + 2 * W * W) + 4 * 2 * ND * W * W
@@ -47,11 +47,12 @@ def tile_graphconvolution_pb_v_kernel(
 
     with ExitStack() as ctx:
         keep = ctx.enter_context(tc.tile_pool(name="keep", bufs=1))
+        slots = ctx.enter_context(tc.tile_pool(name="slots", bufs=3))
+        work = ctx.enter_context(tc.tile_pool(name="work", bufs=2))
         grouped_pool = ctx.enter_context(tc.tile_pool(name="grouped", bufs=4))
-        turned_pool = ctx.enter_context(tc.tile_pool(name="turned", bufs=6))
         result_pool = ctx.enter_context(tc.tile_pool(name="result", bufs=6))
         acc_pool = ctx.enter_context(tc.psum_pool(name="acc", bufs=4))
-        tp_pool = ctx.enter_context(tc.psum_pool(name="tp", bufs=4))
+        turn_pool = ctx.enter_context(tc.psum_pool(name="turn", bufs=4))
         ctx.enter_context(tc.manual_schedule())
 
         ident = keep.tile([P, P], F32, name="ident")
@@ -60,12 +61,22 @@ def tile_graphconvolution_pb_v_kernel(
         nc.vector.memset(warm[:], 0.0)
         nc.scalar.activation(out=warm[:], in_=warm[:], func=ACT.Square)
 
+        x_sb = keep.tile([P, J, W], BF16, name="x_sb")
+        g_sb = keep.tile([P, J, W], BF16, name="g_sb")
+        ds_sb = keep.tile([P, J, W], F32, name="ds_sb")
+        hn_sb = keep.tile([P, J, W], F32, name="hn_sb")
         d_all = keep.tile([P, NG, ND, J, W], BF16, name="d_all")
         d_words = d_all[:].bitcast(F32)
         wih_codes = keep.tile([P, NG, W], U32, name="wih_codes", align_bytes=64)
         wih_scales = keep.tile([P, NG, W], U8, name="wih_scales", align_bytes=64)
         agg_codes = keep.tile([P, ND, W], U32, name="agg_codes", align_bytes=64)
         agg_scales = keep.tile([P, ND, W], U8, name="agg_scales", align_bytes=64)
+        t_codes = keep.tile([P, NG, ND, W], U32, name="t_codes", align_bytes=64)
+        t_scales = keep.tile([P, NG, ND, W], U8, name="t_scales", align_bytes=64)
+
+        c_tiles, z_tiles, r_tiles, e_tiles, hsum_tiles = {}, {}, {}, {}, {}
+        raw_tiles, grouped_tiles = {}, {}
+        banks, turned_tiles, f_codes, f_scales, accs_0, accs_1 = {}, {}, {}, {}, {}, {}
 
         def copy_on(on_vector, out, in_):
             if on_vector:
@@ -73,423 +84,376 @@ def tile_graphconvolution_pb_v_kernel(
             else:
                 nc.scalar.copy(out=out, in_=in_)
 
-        def interleave(on_vector, rows):
-            grouped = grouped_pool.tile([P, ROW], BF16, name="grouped", tag="grouped", align_bytes=64)
+        def interleave(on_vector, grouped, rows):
             copy_on(
                 on_vector,
-                grouped[:].rearrange("p (c i j) -> p c j i", i=4, j=J),
-                rows.rearrange("p j (c i) -> p c j i", i=4),
+                grouped.rearrange("p (c i j) -> p c j i", i=RUN, j=J),
+                rows.rearrange("p j (c i) -> p c j i", i=RUN),
             )
-            return grouped
 
         def quantize(x4, codes, scales, values):
             nc.vector.quantize_mx(out=codes.bitcast(x4), scales=scales, in_=values)
 
-        def transpose_pairs(views):
-            bank = tp_pool.tile([P, W], F32, name="bank", tag="bank")
-            for k, words in enumerate(views):
-                for u in range(2):
-                    nc.tensor.transpose(
-                        out=bank[:, (2 * k + u) * P : (2 * k + u + 1) * P], in_=words[:, u : W // 2 : 2], identity=ident[:]
-                    )
-            return bank
-
-        def copy_pairs(on_vector, bank, n):
-            turned = turned_pool.tile([P, 2 * W], BF16, name="turned", tag="turned", align_bytes=64)
-            copy_on(
-                on_vector,
-                turned[:, 0 : n * W].bitcast(F32).rearrange("q (k r u) -> q k r u", k=n, u=2),
-                bank[:, 0 : n * 2 * P].rearrange("q (k u r) -> q k r u", k=n, u=2),
-            )
-            return turned
-
         def store(on_vector, acc, rows):
-            result = result_pool.tile([P, W], F32, name="result", tag="result")
+            result = result_pool.tile([P, W], F32, name="result")
             copy_on(on_vector, result[:], acc[:])
             nc.sync.dma_start(out=rows, in_=result[:])
 
-        grouped_raw = {}
-        raw_tiles = []
+        def load_gate(out, j, d0, d1, g):
+            nc.sync.dma_start(out=out, in_=gates_v[:, d0:d1, j, g * W : (g + 1) * W])
 
-        def interleave_raw(on_vector, i):
-            grouped_raw[i] = interleave(on_vector, raw_tiles[i][:])
+        def new_slot(j):
+            c_tiles[j] = slots.tile([P, ND, W], F32, name="c_sb")
+            z_tiles[j] = slots.tile([P, ND, W], F32, name="z_sb")
+            r_tiles[j] = slots.tile([P, ND, W], F32, name="r_sb")
+
+        def load_x_c(j):
+            nc.sync.dma_start(out=x_sb[:, j, :], in_=x_v[:, j, :])
+            load_gate(c_tiles[j][:], j, 0, ND, GATE_C)
+
+        def load_z(j):
+            load_gate(z_tiles[j][:], j, 0, ND, GATE_Z)
+
+        def load_g_t(j0, j1):
+            nc.sync.dma_start(out=g_sb[:, j0:j1, :], in_=g_v[:, j0:j1, :])
+            nc.sync.dma_start(out=ds_sb[:, j0:j1, :], in_=t_v[:, j0:j1, :])
+
+        def load_r_hn(j):
+            load_gate(r_tiles[j][:], j, 0, ND, GATE_R)
+            nc.sync.dma_start(out=hn_sb[:, j, :], in_=hn_v[:, j, :])
+
+        def load_raw(i):
+            raw_tiles[i] = grouped_pool.tile([P, J, W], BF16, name="raw")
+            nc.sync.dma_start(out=raw_tiles[i][:], in_=wih_v[i] if i < NG else agg_v[i - NG])
+
+        def group_raw(i):
+            grouped_tiles[i] = grouped_pool.tile([P, ROW], BF16, name="grouped", align_bytes=64)
+            interleave(False, grouped_tiles[i][:], raw_tiles[i][:])
 
         def quantize_raw(i):
             if i < NG:
-                quantize(E4M3X4, wih_codes[:, i, :], wih_scales[:, i, :], grouped_raw[i][:])
+                quantize(E4M3X4, wih_codes[:, i, :], wih_scales[:, i, :], grouped_tiles[i][:])
             else:
-                quantize(E4M3X4, agg_codes[:, i - NG, :], agg_scales[:, i - NG, :], grouped_raw[i][:])
+                quantize(E4M3X4, agg_codes[:, i - NG, :], agg_scales[:, i - NG, :], grouped_tiles[i][:])
 
-        with tc.tile_pool(name="stage1", bufs=1) as s1:
-            x_sb = s1.tile([P, J, W], BF16, name="x_sb")
-            g_sb = s1.tile([P, J, W], BF16, name="g_sb")
-            ds_sb = s1.tile([P, J, W], F32, name="ds_sb")
-            hn_sb = s1.tile([P, J, W], F32, name="hn_sb")
-            c_tiles, z_tiles, r_tiles, e_tiles, hsum_tiles, f_codes, f_scales = {}, {}, {}, {}, {}, {}, {}
-            banks, turned = {}, {}
-            accs = {}
+        def h_minus_c(j, d0, d1):
+            nc.vector.tensor_tensor(
+                out=e_tiles[j][:, d0:d1, :],
+                in0=x_sb[:, j : j + 1, :].to_broadcast([P, d1 - d0, W]),
+                in1=c_tiles[j][:, d0:d1, :],
+                op=ALU.subtract,
+            )
 
-            def load_gate(out, j, d0, d1, g):
-                nc.sync.dma_start(out=out, in_=gates_v[:, d0:d1, j, g * W : (g + 1) * W])
+        def times_z(j, d0, d1):
+            nc.vector.tensor_tensor(
+                out=e_tiles[j][:, d0:d1, :], in0=z_tiles[j][:, d0:d1, :], in1=e_tiles[j][:, d0:d1, :], op=ALU.mult
+            )
 
-            def alloc_slot(j):
-                c_tiles[j] = s1.tile([P, ND, W], F32, name="c_sb", tag="c_sb", bufs=3)
-                z_tiles[j] = s1.tile([P, ND, W], F32, name="z_sb", tag="z_sb", bufs=3)
-                r_tiles[j] = s1.tile([P, ND, W], F32, name="r_sb", tag="r_sb", bufs=3)
+        def add_to_hsum(j, term, start, stop):
+            nc.tensor.matmul(out=hsum_tiles[j][:], lhsT=ident[:], rhs=term, start=start, stop=stop)
 
-            def load_x_c(j):
-                nc.sync.dma_start(out=x_sb[:, j, :], in_=x_v[:, j, :])
-                load_gate(c_tiles[j][:], j, 0, ND, GATE_C)
+        def start_e(j):
+            e_tiles[j] = work.tile([P, ND, W], F32, name="e_sb")
+            h_minus_c(j, 0, ND)
 
-            def load_g_t(j):
-                nc.sync.dma_start(out=g_sb[:, j, :], in_=g_v[:, j, :])
-                nc.sync.dma_start(out=ds_sb[:, j, :], in_=t_v[:, j, :])
-
-            def load_r_hn(j):
-                load_gate(r_tiles[j][:], j, 0, ND, GATE_R)
-                nc.sync.dma_start(out=hn_sb[:, j, :], in_=hn_v[:, j, :])
-
-            def load_raw(i):
-                raw_tiles.append(s1.tile([P, J, W], BF16, name="raw", tag="raw", bufs=RAW_BUFS))
-                nc.sync.dma_start(out=raw_tiles[i][:], in_=wih_v[i] if i < NG else agg_v[i - NG])
-
-            def load_slot(j):
-                alloc_slot(j)
-                load_x_c(j)
-                load_gate(z_tiles[j][:], j, 0, ND, GATE_Z)
-                load_g_t(j)
-                load_r_hn(j)
-
-            alloc_slot(0)
-            nc.sync.dma_start(out=x_sb[:, 0, :], in_=x_v[:, 0, :])
+        def add_c(j):
+            hsum_tiles[j] = acc_pool.tile([P, W], F32, name="acc")
             for d in range(ND):
-                load_gate(c_tiles[0][:, d : d + 1, :], 0, d, d + 1, GATE_C)
-                load_gate(z_tiles[0][:, d : d + 1, :], 0, d, d + 1, GATE_Z)
-            alloc_slot(1)
-            load_x_c(1)
-            load_g_t(0)
-            load_gate(z_tiles[1][:], 1, 0, ND, GATE_Z)
-            load_raw(0)
-            load_r_hn(0)
-            alloc_slot(2)
-            load_x_c(2)
-            load_raw(1)
-            load_g_t(1)
-            load_gate(z_tiles[2][:], 2, 0, ND, GATE_Z)
-            load_raw(2)
-            load_r_hn(1)
-            load_g_t(2)
-            load_r_hn(2)
-            load_raw(3)
+                add_to_hsum(j, c_tiles[j][:, d, :], d == 0, False)
 
-            def new_slot(j):
-                e_tiles[j] = s1.tile([P, ND, W], F32, name="e_sb", tag="e_sb", bufs=2)
+        def times_z_and_add(j):
+            times_z(j, 0, ND)
+            for d in range(ND):
+                add_to_hsum(j, e_tiles[j][:, d, :], False, d == ND - 1)
 
-            def h_minus_c(j, d0, d1):
-                nc.vector.tensor_tensor(
-                    out=e_tiles[j][:, d0:d1, :],
-                    in0=x_sb[:, j : j + 1, :].to_broadcast([P, d1 - d0, W]),
-                    in1=c_tiles[j][:, d0:d1, :],
-                    op=ALU.subtract,
-                )
+        def square_c(j):
+            nc.scalar.activation(out=c_tiles[j][:], in_=c_tiles[j][:], func=ACT.Square)
 
-            def times_z(j, d0, d1):
-                nc.vector.tensor_tensor(
-                    out=e_tiles[j][:, d0:d1, :], in0=z_tiles[j][:, d0:d1, :], in1=e_tiles[j][:, d0:d1, :], op=ALU.mult
-                )
+        def square_r(j):
+            nc.scalar.activation(out=r_tiles[j][:], in_=r_tiles[j][:], func=ACT.Square, bias=-0.5, scale=1.0)
 
-            def add_to_hsum(j, term, start, stop):
-                nc.tensor.matmul(out=hsum_tiles[j][:], lhsT=ident[:], rhs=term, start=start, stop=stop)
+        def grad_times_t(j0, j1):
+            nc.vector.tensor_tensor(out=ds_sb[:, j0:j1, :], in0=g_sb[:, j0:j1, :], in1=ds_sb[:, j0:j1, :], op=ALU.mult)
 
-            def add_c(j):
-                hsum_tiles[j] = acc_pool.tile([P, W], F32, name="hsum", tag="acc")
-                for d in range(ND):
-                    add_to_hsum(j, c_tiles[j][:, d, :], d == 0, False)
+        def make_ds(j):
+            nc.vector.scalar_tensor_tensor(
+                out=ds_sb[:, j, :], in0=hsum_tiles[j][:], scalar=0.0, in1=ds_sb[:, j, :], op0=ALU.is_gt, op1=ALU.mult
+            )
 
-            def add_ze(j):
-                for d in range(ND):
-                    add_to_hsum(j, e_tiles[j][:, d, :], False, d == ND - 1)
+        def z_minus_1_times_ds(j):
+            nc.vector.scalar_tensor_tensor(
+                out=z_tiles[j][:], in0=z_tiles[j][:], scalar=1.0, in1=ds_sb[:, j : j + 1, :].to_broadcast([P, ND, W]),
+                op0=ALU.subtract, op1=ALU.mult,
+            )
 
-            def square_c(j):
-                nc.scalar.activation(out=c_tiles[j][:], in_=c_tiles[j][:], func=ACT.Square)
+        def make_dz(j):
+            nc.vector.scalar_tensor_tensor(
+                out=d_all[:, DZ, :, j, :], in0=e_tiles[j][:], scalar=-1.0, in1=z_tiles[j][:], op0=ALU.mult, op1=ALU.mult
+            )
 
-            def square_r(j):
-                nc.scalar.activation(out=r_tiles[j][:], in_=r_tiles[j][:], func=ACT.Square, bias=-0.5, scale=1.0)
+        def make_dc(j):
+            nc.vector.scalar_tensor_tensor(
+                out=c_tiles[j][:], in0=c_tiles[j][:], scalar=1.0, in1=z_tiles[j][:], op0=ALU.subtract, op1=ALU.mult
+            )
 
-            def grad_times_t(j):
-                nc.vector.tensor_tensor(out=ds_sb[:, j, :], in0=g_sb[:, j, :], in1=ds_sb[:, j, :], op=ALU.mult)
+        def round_dc(j):
+            nc.scalar.copy(out=d_all[:, DC, :, j, :], in_=c_tiles[j][:])
 
-            def mask(j):
-                nc.vector.scalar_tensor_tensor(
-                    out=ds_sb[:, j, :], in0=hsum_tiles[j][:], scalar=0.0, in1=ds_sb[:, j, :], op0=ALU.is_gt, op1=ALU.mult
-                )
+        def dc_times_r_terms(j):
+            nc.vector.scalar_tensor_tensor(
+                out=r_tiles[j][:], in0=r_tiles[j][:], scalar=0.25, in1=c_tiles[j][:], op0=ALU.subtract, op1=ALU.mult
+            )
 
-            def a_op(j):
-                nc.vector.scalar_tensor_tensor(
-                    out=z_tiles[j][:], in0=z_tiles[j][:], scalar=1.0, in1=ds_sb[:, j : j + 1, :].to_broadcast([P, ND, W]),
-                    op0=ALU.subtract, op1=ALU.mult,
-                )
+        def make_dr(j):
+            nc.vector.scalar_tensor_tensor(
+                out=d_all[:, DR, :, j, :], in0=r_tiles[j][:], scalar=-1.0,
+                in1=hn_sb[:, j : j + 1, :].to_broadcast([P, ND, W]), op0=ALU.mult, op1=ALU.mult,
+            )
 
-            def dz_op(j):
-                nc.vector.scalar_tensor_tensor(
-                    out=d_all[:, 1, :, j, :], in0=e_tiles[j][:], scalar=-1.0, in1=z_tiles[j][:], op0=ALU.mult, op1=ALU.mult
-                )
+        def block_words(j, k):
+            if k < 2 * ND:
+                return d_words[:, k % 2, k // 2, j, :]
+            return d_words[:, DR, k - 2 * ND, j, :]
 
-            def dc_op(j):
-                nc.vector.scalar_tensor_tensor(
-                    out=c_tiles[j][:], in0=c_tiles[j][:], scalar=1.0, in1=z_tiles[j][:], op0=ALU.subtract, op1=ALU.mult
-                )
+        def blocks_of(b):
+            return range(2 * b, min(2 * b + 2, NG * ND))
 
-            def cast_dc(j):
-                nc.scalar.copy(out=d_all[:, 0, :, j, :], in_=c_tiles[j][:])
+        def turn(j, b):
+            banks[(j, b)] = turn_pool.tile([P, W], F32, name="bank")
+            for i, k in enumerate(blocks_of(b)):
+                for u in range(2):
+                    nc.tensor.transpose(
+                        out=banks[(j, b)][:, (2 * i + u) * P : (2 * i + u + 1) * P],
+                        in_=block_words(j, k)[:, u : W // 2 : 2],
+                        identity=ident[:],
+                    )
 
-            def b_op(j):
-                nc.vector.scalar_tensor_tensor(
-                    out=r_tiles[j][:], in0=r_tiles[j][:], scalar=0.25, in1=c_tiles[j][:], op0=ALU.subtract, op1=ALU.mult
-                )
+        def new_turned(j):
+            turned_tiles[j] = work.tile([P, NG * ND * W], BF16, name="turned", bufs=1, align_bytes=64)
+            f_codes[j] = work.tile([P, NG * ND * P], U32, name="f_codes", align_bytes=64)
+            f_scales[j] = work.tile([P, NG * ND * P], U8, name="f_scales", align_bytes=64)
 
-            def dr_op(j):
-                nc.vector.scalar_tensor_tensor(
-                    out=d_all[:, 2, :, j, :], in0=r_tiles[j][:], scalar=-1.0,
-                    in1=hn_sb[:, j : j + 1, :].to_broadcast([P, ND, W]), op0=ALU.mult, op1=ALU.mult,
-                )
+        def copy_turned(j, b):
+            n = len(blocks_of(b))
+            nc.scalar.copy(
+                out=turned_tiles[j][:, 2 * b * W : (2 * b + n) * W].bitcast(F32).rearrange("q (k r u) -> q k r u", k=n, u=2),
+                in_=banks[(j, b)][:, 0 : n * 2 * P].rearrange("q (k u r) -> q k r u", k=n, u=2),
+            )
 
-            def turn_cz(j):
-                for d in range(ND):
-                    banks[(j, d)] = transpose_pairs([d_words[:, 0, d, j, :], d_words[:, 1, d, j, :]])
+        def quantize_turned(j, k0, k1):
+            quantize(E5M2X4, f_codes[j][:, k0 * P : k1 * P], f_scales[j][:, k0 * P : k1 * P], turned_tiles[j][:, k0 * W : k1 * W])
 
-            def turn_r(j):
-                banks[(j, 3)] = transpose_pairs([d_words[:, 2, 0, j, :], d_words[:, 2, 1, j, :]])
-                banks[(j, 4)] = transpose_pairs([d_words[:, 2, 2, j, :]])
-
-            def copy_turned(on_vector, j, i):
-                turned[(j, i)] = copy_pairs(on_vector, banks[(j, i)], 1 if i == 4 else 2)
-
-            def quantize_turned(j, i):
-                if i == 0:
-                    f_codes[j] = s1.tile([P, 9 * P], U32, name="f_codes", tag="f_codes", bufs=2, align_bytes=64)
-                    f_scales[j] = s1.tile([P, 9 * P], U8, name="f_scales", tag="f_scales", bufs=2, align_bytes=64)
-                n = 1 if i == 4 else 2
-                quantize(
-                    E5M2X4, f_codes[j][:, i * 2 * P : (i * 2 + n) * P], f_scales[j][:, i * 2 * P : (i * 2 + n) * P],
-                    turned[(j, i)][:, 0 : n * W],
-                )
-
-            def mm0(d, j):
-                acc = acc_pool.tile([P, W], F32, name="acc0", tag="acc")
-                accs[(d, j)] = acc
-                for i, (col, g) in enumerate(((2 * d, GATE_C), (2 * d + 1, GATE_Z), (6 + d, GATE_R))):
+        def multiply_0(j):
+            for d in range(ND):
+                accs_0[(d, j)] = acc_pool.tile([P, W], F32, name="acc")
+                for i, (k, g) in enumerate(((2 * d, GATE_C), (2 * d + 1, GATE_Z), (2 * ND + d, GATE_R))):
                     nc.tensor.matmul_mx(
-                        out=acc[:], lhsT=f_codes[j][:, col * P : (col + 1) * P].bitcast(E5M2X4),
-                        lhsT_scale=f_scales[j][:, col * P : (col + 1) * P],
+                        out=accs_0[(d, j)][:],
+                        lhsT=f_codes[j][:, k * P : (k + 1) * P].bitcast(E5M2X4), lhsT_scale=f_scales[j][:, k * P : (k + 1) * P],
                         rhs=wih_codes[:, g, :].bitcast(E4M3X4), rhs_scale=wih_scales[:, g, :],
                         start=(i == 0), stop=(i == NG - 1),
                     )
 
-            def out0(on_vector, d, j):
-                store(on_vector, accs[(d, j)], out0_v[d][:, j, :])
+        def store_0(j):
+            for d in range(ND):
+                store(False, accs_0[(d, j)], out0_v[d][:, j, :])
 
-            new_slot(0)
-            hsum_tiles[0] = acc_pool.tile([P, W], F32, name="hsum", tag="acc")
-            h_minus_c(0, 0, 1)
-            add_to_hsum(0, c_tiles[0][:, 0, :], True, False)
-            h_minus_c(0, 1, 2)
-            add_to_hsum(0, c_tiles[0][:, 1, :], False, False)
-            times_z(0, 0, 1)
-            add_to_hsum(0, e_tiles[0][:, 0, :], False, False)
-            h_minus_c(0, 2, 3)
-            add_to_hsum(0, c_tiles[0][:, 2, :], False, False)
-            times_z(0, 1, 2)
-            add_to_hsum(0, e_tiles[0][:, 1, :], False, False)
-            times_z(0, 2, 3)
-            add_to_hsum(0, e_tiles[0][:, 2, :], False, True)
-            new_slot(1)
-            h_minus_c(1, 0, ND)
-            square_c(0)
-            grad_times_t(0)
+        def rows_of(g, d):
+            return d_all[:, DR - g, d, :, :]
 
-            t_codes = keep.tile([P, NG, ND, W], U32, name="t_codes", align_bytes=64)
-            t_scales = keep.tile([P, NG, ND, W], U8, name="t_scales", align_bytes=64)
-            grouped_t = {}
-            accs1 = {}
+        def group_t(on_vector, g, d, m0, m1):
+            if m0 == 0:
+                grouped_tiles[(g, d)] = grouped_pool.tile([P, ROW], BF16, name="grouped", align_bytes=64)
+            interleave(on_vector, grouped_tiles[(g, d)][:, m0 * J * P : m1 * J * P], rows_of(g, d)[:, :, m0 * P : m1 * P])
 
-            def group_t(on_vector, g, d):
-                grouped_t[(g, d)] = interleave(on_vector, d_all[:, 2 - g, d, :, :])
+        def quantize_t(g, d, m0, m1):
+            quantize(
+                E5M2X4, t_codes[:, g, d, m0 * P : m1 * P], t_scales[:, g, d, m0 * P : m1 * P],
+                grouped_tiles[(g, d)][:, m0 * J * P : m1 * J * P],
+            )
 
-            def group_part(g, d, m):
-                if m == 0:
-                    grouped_t[(g, d)] = grouped_pool.tile([P, ROW], BF16, name="grouped", tag="grouped", align_bytes=64)
-                nc.vector.tensor_copy(
-                    out=grouped_t[(g, d)][:, m * J * P : (m + 1) * J * P].rearrange("p (c i j) -> p c j i", i=4, j=J),
-                    in_=d_all[:, 2 - g, d, :, m * P : (m + 1) * P].rearrange("p j (c i) -> p c j i", i=4),
+        def multiply_1(g, m, d0, d1):
+            if d0 == 0 and g == GATE_C:
+                accs_1[(g, m)] = acc_pool.tile([P, W], F32, name="acc")
+            elif d0 == 0:
+                accs_1[(g, m)] = turn_pool.tile([P, W], F32, name="bank")
+            for d in range(d0, d1):
+                nc.tensor.matmul_mx(
+                    out=accs_1[(g, m)][:],
+                    lhsT=t_codes[:, g, d, m * P : (m + 1) * P].bitcast(E5M2X4), lhsT_scale=t_scales[:, g, d, m * P : (m + 1) * P],
+                    rhs=agg_codes[:, d, :].bitcast(E4M3X4), rhs_scale=agg_scales[:, d, :],
+                    start=(d == 0), stop=(d == ND - 1),
                 )
 
-            def quantize_part(g, d, m):
-                quantize(
-                    E5M2X4, t_codes[:, g, d, m * P : (m + 1) * P], t_scales[:, g, d, m * P : (m + 1) * P],
-                    grouped_t[(g, d)][:, m * J * P : (m + 1) * J * P],
-                )
+        def store_1(on_vector, g, m):
+            store(on_vector, accs_1[(g, m)], out1_v[g * J + m])
 
-            def quantize_t(g, d):
-                quantize(E5M2X4, t_codes[:, g, d, :], t_scales[:, g, d, :], grouped_t[(g, d)][:])
+        new_slot(0)
+        nc.sync.dma_start(out=x_sb[:, 0, :], in_=x_v[:, 0, :])
+        for d in range(ND):
+            load_gate(c_tiles[0][:, d : d + 1, :], 0, d, d + 1, GATE_C)
+            load_gate(z_tiles[0][:, d : d + 1, :], 0, d, d + 1, GATE_Z)
+        new_slot(1)
+        load_x_c(1)
+        load_g_t(0, 1)
+        load_z(1)
+        load_raw(0)
+        load_r_hn(0)
+        new_slot(2)
+        load_x_c(2)
+        load_raw(1)
+        load_g_t(1, J)
+        load_z(2)
+        load_raw(2)
+        load_r_hn(1)
 
-            def mm1(g, m, d0, d1):
-                if d0 == 0 and g == GATE_C:
-                    accs1[(g, m)] = acc_pool.tile([P, W], F32, name="acc1", tag="acc")
-                elif d0 == 0:
-                    accs1[(g, m)] = tp_pool.tile([P, W], F32, name="bank", tag="bank")
-                for d in range(d0, d1):
-                    nc.tensor.matmul_mx(
-                        out=accs1[(g, m)][:],
-                        lhsT=t_codes[:, g, d, m * P : (m + 1) * P].bitcast(E5M2X4),
-                        lhsT_scale=t_scales[:, g, d, m * P : (m + 1) * P],
-                        rhs=agg_codes[:, d, :].bitcast(E4M3X4), rhs_scale=agg_scales[:, d, :],
-                        start=(d == 0), stop=(d == ND - 1),
-                    )
+        e_tiles[0] = work.tile([P, ND, W], F32, name="e_sb")
+        hsum_tiles[0] = acc_pool.tile([P, W], F32, name="acc")
+        h_minus_c(0, 0, 1)
+        add_to_hsum(0, c_tiles[0][:, 0, :], True, False)
+        h_minus_c(0, 1, 2)
+        add_to_hsum(0, c_tiles[0][:, 1, :], False, False)
+        times_z(0, 0, 1)
+        add_to_hsum(0, e_tiles[0][:, 0, :], False, False)
+        h_minus_c(0, 2, 3)
+        add_to_hsum(0, c_tiles[0][:, 2, :], False, False)
+        times_z(0, 1, 2)
+        add_to_hsum(0, e_tiles[0][:, 1, :], False, False)
+        times_z(0, 2, 3)
+        add_to_hsum(0, e_tiles[0][:, 2, :], False, True)
+        start_e(1)
+        square_c(0)
+        grad_times_t(0, 1)
 
-            def out1(on_vector, g, m):
-                store(on_vector, accs1[(g, m)], out1_v[g * J + m])
+        spare = [0, 1, 2, 3, 4, 5]
 
+        def use_spare_time(n):
+            for i in range(n):
+                group_raw(spare.pop(0))
 
-            spare = [lambda i=i: interleave_raw(False, i) for i in range(NG + ND)]
-            for j in range(J - 1):
-                mask(j)
-                if j + 1 < J:
-                    add_c(j + 1)
-                if j > 0:
-                    copy_turned(False, j - 1, 3)
-                    copy_turned(False, j - 1, 4)
-                    quantize_turned(j - 1, 0)
-                a_op(j)
-                if j > 0:
-                    quantize_turned(j - 1, 1)
-                if j + 1 < J:
-                    times_z(j + 1, 0, ND)
-                    add_ze(j + 1)
-                if j > 0:
-                    quantize_turned(j - 1, 2)
-                if j + 1 < J:
-                    dz_op(j)
-                else:
-                    dc_op(j)
-                if j > 0:
-                    quantize_turned(j - 1, 3)
-                if j + 1 < J:
-                    dc_op(j)
-                else:
-                    dz_op(j)
-                if j > 0:
-                    quantize_turned(j - 1, 4)
-                if j > 1:
-                    for d in range(ND):
-                        mm0(d, j - 1)
-                for i in range(SPARE_A[j]):
-                    spare.pop(0)()
-                square_r(j)
-                if j + 1 < J:
-                    square_c(j + 1)
-                for i in range(SPARE_B[j]):
-                    spare.pop(0)()
-                cast_dc(j)
-                turn_cz(j)
-                if j + 2 < J:
-                    new_slot(j + 2)
-                    h_minus_c(j + 2, 0, ND)
-                b_op(j)
-                if j + 1 < J:
-                    grad_times_t(j + 1)
-                dr_op(j)
-                for i in range(SPARE_C[j]):
-                    spare.pop(0)()
-                if j > 1:
-                    for d in range(ND):
-                        out0(False, d, j - 1)
-                for i in range(3):
-                    copy_turned(False, j, i)
-                turn_r(j)
-                for i in QRAW[j]:
-                    quantize_raw(i)
-                for i in range(SPARE_D[j]):
-                    spare.pop(0)()
-                if j == 1:
-                    for d in range(ND):
-                        mm0(d, 0)
-                    for d in range(ND):
-                        out0(False, d, 0)
-                if j == 0:
-                    load_raw(4)
-                    load_raw(5)
-                    load_slot(3)
+        for j in range(LAST):
+            make_ds(j)
+            add_c(j + 1)
+            if j > 0:
+                copy_turned(j - 1, 3)
+                copy_turned(j - 1, 4)
+                quantize_turned(j - 1, 0, 4)
+            z_minus_1_times_ds(j)
+            times_z_and_add(j + 1)
+            make_dz(j)
+            if j > 0:
+                quantize_turned(j - 1, 4, 8)
+            make_dc(j)
+            if j > 0:
+                quantize_turned(j - 1, 8, 9)
+            if j == 2:
+                multiply_0(j - 1)
+            use_spare_time(SPARE_A[j])
+            square_r(j)
+            square_c(j + 1)
+            use_spare_time(SPARE_B[j])
+            round_dc(j)
+            new_turned(j)
+            for b in range(3):
+                turn(j, b)
+            if j + 2 < J:
+                start_e(j + 2)
+            dc_times_r_terms(j)
+            if j == 0:
+                grad_times_t(1, J)
+            else:
+                quantize_raw(3 * (j - 1))
+            make_dr(j)
+            use_spare_time(SPARE_C[j])
+            if j == 2:
+                store_0(j - 1)
+            for b in range(3):
+                copy_turned(j, b)
+            turn(j, 3)
+            turn(j, 4)
+            if j == 0:
+                new_slot(LAST)
+                load_x_c(LAST)
+                load_z(LAST)
+                load_r_hn(2)
+                load_raw(3)
+                load_raw(4)
+                load_raw(5)
+                load_r_hn(LAST)
+            if j == 1:
+                quantize_raw(1)
+                quantize_raw(2)
+                use_spare_time(1)
+                multiply_0(0)
+                store_0(0)
+            if j == 2:
+                quantize_raw(4)
 
-
-            L = J - 1
-            mask(L)
-            copy_turned(False, L - 1, 3)
-            copy_turned(False, L - 1, 4)
-            quantize_turned(L - 1, 0)
-            a_op(L)
-            quantize_turned(L - 1, 1)
-            dc_op(L)
-            square_r(L)
-            cast_dc(L)
-            quantize_turned(L - 1, 2)
-            dz_op(L)
-            quantize_turned(L - 1, 3)
-            quantize_turned(L - 1, 4)
-            for d in range(ND):
-                mm0(d, L - 1)
-            turn_cz(L)
-            b_op(L)
-            group_t(False, GATE_C, 0)
-            quantize_raw(5)
-            dr_op(L)
-            for d in range(ND):
-                out0(False, d, L - 1)
-            for i in range(3):
-                copy_turned(False, L, i)
-            turn_r(L)
-            copy_turned(False, L, 3)
-            copy_turned(False, L, 4)
-            group_t(True, GATE_Z, 0)
-            group_t(True, GATE_Z, 1)
-            for i in range(5):
-                quantize_turned(L, i)
-            for d in range(ND):
-                mm0(d, L)
-            quantize_t(GATE_C, 0)
-            group_t(False, GATE_C, 1)
-            quantize_t(GATE_Z, 0)
-            group_t(True, GATE_Z, 2)
-            quantize_t(GATE_Z, 1)
-            quantize_t(GATE_Z, 2)
-            for d in range(ND):
-                for m in range(J):
-                    mm1(GATE_Z, m, d, d + 1)
-            group_t(False, GATE_C, 2)
-            quantize_t(GATE_C, 1)
-            group_t(True, GATE_R, 0)
-            quantize_t(GATE_C, 2)
-            for d in range(ND):
-                out0(False, d, L)
+        make_ds(LAST)
+        copy_turned(LAST - 1, 3)
+        copy_turned(LAST - 1, 4)
+        quantize_turned(LAST - 1, 0, 4)
+        z_minus_1_times_ds(LAST)
+        quantize_turned(LAST - 1, 4, 8)
+        make_dc(LAST)
+        square_r(LAST)
+        round_dc(LAST)
+        quantize_turned(LAST - 1, 8, 9)
+        make_dz(LAST)
+        multiply_0(LAST - 1)
+        new_turned(LAST)
+        for b in range(3):
+            turn(LAST, b)
+        dc_times_r_terms(LAST)
+        group_t(False, GATE_C, 0, 0, J)
+        quantize_raw(5)
+        make_dr(LAST)
+        store_0(LAST - 1)
+        for b in range(3):
+            copy_turned(LAST, b)
+        turn(LAST, 3)
+        turn(LAST, 4)
+        copy_turned(LAST, 3)
+        copy_turned(LAST, 4)
+        group_t(True, GATE_Z, 0, 0, J)
+        group_t(True, GATE_Z, 1, 0, J)
+        quantize_turned(LAST, 0, 4)
+        quantize_turned(LAST, 4, 8)
+        quantize_turned(LAST, 8, 9)
+        multiply_0(LAST)
+        quantize_t(GATE_C, 0, 0, J)
+        group_t(False, GATE_C, 1, 0, J)
+        quantize_t(GATE_Z, 0, 0, J)
+        group_t(True, GATE_Z, 2, 0, J)
+        quantize_t(GATE_Z, 1, 0, J)
+        quantize_t(GATE_Z, 2, 0, J)
+        for d in range(ND):
             for m in range(J):
-                mm1(GATE_C, m, 0, ND)
-            for m in range(J):
-                out1(False, GATE_Z, m)
-            group_t(True, GATE_R, 1)
-            quantize_t(GATE_R, 0)
-            for m in range(J):
-                mm1(GATE_R, m, 0, 1)
-            group_part(GATE_R, 2, 0)
-            quantize_t(GATE_R, 1)
-            for m in range(J):
-                mm1(GATE_R, m, 1, 2)
-            for m in range(J):
-                out1(False, GATE_C, m)
-            group_part(GATE_R, 2, 1)
-            for m in range(J):
-                quantize_part(GATE_R, 2, m)
-                if m + 2 < J:
-                    group_part(GATE_R, 2, m + 2)
-                mm1(GATE_R, m, 2, 3)
-            for m in range(J):
-                out1(m % 2 == 1, GATE_R, m)
+                multiply_1(GATE_Z, m, d, d + 1)
+        group_t(False, GATE_C, 2, 0, J)
+        quantize_t(GATE_C, 1, 0, J)
+        group_t(True, GATE_R, 0, 0, J)
+        quantize_t(GATE_C, 2, 0, J)
+        store_0(LAST)
+        for m in range(J):
+            multiply_1(GATE_C, m, 0, ND)
+        for m in range(J):
+            store_1(False, GATE_Z, m)
+        group_t(True, GATE_R, 1, 0, J)
+        quantize_t(GATE_R, 0, 0, J)
+        for m in range(J):
+            multiply_1(GATE_R, m, 0, 1)
+        group_t(True, GATE_R, 2, 0, 1)
+        quantize_t(GATE_R, 1, 0, J)
+        for m in range(J):
+            multiply_1(GATE_R, m, 1, 2)
+        for m in range(J):
+            store_1(False, GATE_C, m)
+        group_t(True, GATE_R, 2, 1, 2)
+        for m in range(J):
+            quantize_t(GATE_R, 2, m, m + 1)
+            if m + 2 < J:
+                group_t(True, GATE_R, 2, m + 2, m + 3)
+            multiply_1(GATE_R, m, 2, 3)
+        for m in range(J):
+            store_1(m % 2 == 1, GATE_R, m)

@@ -50,7 +50,7 @@ def tile_graphconvolution_pb_v_kernel(
         slots = ctx.enter_context(tc.tile_pool(name="slots", bufs=3))
         work = ctx.enter_context(tc.tile_pool(name="work", bufs=2))
         grouped_pool = ctx.enter_context(tc.tile_pool(name="grouped", bufs=4))
-        result_pool = ctx.enter_context(tc.tile_pool(name="result", bufs=6))
+        result_pool = ctx.enter_context(tc.tile_pool(name="result", bufs=8))
         acc_pool = ctx.enter_context(tc.psum_pool(name="acc", bufs=4))
         turn_pool = ctx.enter_context(tc.psum_pool(name="turn", bufs=4))
         ctx.enter_context(tc.manual_schedule())
@@ -441,12 +441,8 @@ def tile_graphconvolution_pb_v_kernel(
             store_1(False, GATE_Z, m)
         group_t(True, GATE_R, 1, 0, J)
         quantize_t(GATE_R, 0, 0, J)
-        for m in range(J):
-            multiply_1(GATE_R, m, 0, 1)
         group_t(True, GATE_R, 2, 0, 1)
         quantize_t(GATE_R, 1, 0, J)
-        for m in range(J):
-            multiply_1(GATE_R, m, 1, 2)
         for m in range(J):
             store_1(False, GATE_C, m)
         group_t(True, GATE_R, 2, 1, 2)
@@ -454,6 +450,7 @@ def tile_graphconvolution_pb_v_kernel(
             quantize_t(GATE_R, 2, m, m + 1)
             if m + 2 < J:
                 group_t(True, GATE_R, 2, m + 2, m + 3)
-            multiply_1(GATE_R, m, 2, 3)
-        for m in range(J):
-            store_1(m % 2 == 1, GATE_R, m)
+            multiply_1(GATE_R, m, 0, ND)
+            if m < LAST:
+                store_1(False, GATE_R, m)
+        store_1(True, GATE_R, LAST)

from contextlib import ExitStack

import concourse.masks as masks
import concourse.mybir as mybir

F32 = mybir.dt.float32
BF16 = mybir.dt.bfloat16
U32 = mybir.dt.uint32
U8 = mybir.dt.uint8
E4M3X4 = mybir.dt.float8_e4m3fn_x4
E5M2X4 = mybir.dt.float8_e5m2_x4
ALU = mybir.AluOpType
ACT = mybir.ActivationFunctionType

P = 128
J = 4
W = 512
ND = 3
NG = 3
ROW = J * W
GATE_R, GATE_Z, GATE_C = 0, 1, 2
DC, DZ, DR = 0, 1, 2
LAST = J - 1
SPARE_A = (1, 0, 0)
SPARE_B = (0, 1, 1)
SPARE_C = (1, 1, 0)
RUN = 8

FLOPS = 2 * 2 * (ND * W) * (NG * W) * W
BYTES = 2 * (ND * W * W + W * W + NG * W * W + W * W) + 4 * (ND * W * NG * W + 2 * W * W) + 4 * 2 * ND * W * W


def tile_graphconvolution_pb_v_kernel(
    tc, agg, x, wih, whh, bih, bhh, wh, bh, gates, hn, t, grad_out, out_0, out_1
):
    nc = tc.nc

    gates_v = gates[:, 0, :, :].rearrange("d (p j) f -> p d j f", j=J)
    x_v = x[:, 0, :].rearrange("(p j) w -> p j w", j=J)
    g_v = grad_out[:, 0, :].rearrange("(p j) w -> p j w", j=J)
    t_v = t[:, 0, :].rearrange("(p j) w -> p j w", j=J)
    hn_v = hn[0, :, :].rearrange("(p j) w -> p j w", j=J)
    agg_v = agg[:, 0, :, :].rearrange("d (p j) w -> d p j w", j=J)
    wih_v = wih.rearrange("(g p j) c -> g p j c", g=NG, j=J)
    out0_v = out_0[:, 0, :, :].rearrange("d (p j) w -> d p j w", j=J)
    out1_v = out_1.rearrange("(m p) c -> m p c", p=P)

    with ExitStack() as ctx:
        keep = ctx.enter_context(tc.tile_pool(name="keep", bufs=1))
        slots = ctx.enter_context(tc.tile_pool(name="slots", bufs=3))
        work = ctx.enter_context(tc.tile_pool(name="work", bufs=2))
        grouped_pool = ctx.enter_context(tc.tile_pool(name="grouped", bufs=4))
        result_pool = ctx.enter_context(tc.tile_pool(name="result", bufs=8))
        acc_pool = ctx.enter_context(tc.psum_pool(name="acc", bufs=4))
        turn_pool = ctx.enter_context(tc.psum_pool(name="turn", bufs=4))
        ctx.enter_context(tc.manual_schedule())

        ident = keep.tile([P, P], F32, name="ident")
        masks.make_identity(nc, ident[:])
        warm = keep.tile([P, 1], F32, name="warm")
        nc.vector.memset(warm[:], 0.0)
        nc.scalar.activation(out=warm[:], in_=warm[:], func=ACT.Square)

        x_sb = keep.tile([P, J, W], BF16, name="x_sb")
        g_sb = keep.tile([P, J, W], BF16, name="g_sb")
        ds_sb = keep.tile([P, J, W], F32, name="ds_sb")
        hn_sb = keep.tile([P, J, W], F32, name="hn_sb")
        d_all = keep.tile([P, NG, ND, J, W], BF16, name="d_all")
        d_words = d_all[:].bitcast(F32)
        wih_codes = keep.tile([P, NG, W], U32, name="wih_codes", align_bytes=64)
        wih_scales = keep.tile([P, NG, W], U8, name="wih_scales", align_bytes=64)
        agg_codes = keep.tile([P, ND, W], U32, name="agg_codes", align_bytes=64)
        agg_scales = keep.tile([P, ND, W], U8, name="agg_scales", align_bytes=64)
        t_codes = keep.tile([P, NG, ND, W], U32, name="t_codes", align_bytes=64)
        t_scales = keep.tile([P, NG, ND, W], U8, name="t_scales", align_bytes=64)

        c_tiles, z_tiles, r_tiles, e_tiles, hsum_tiles = {}, {}, {}, {}, {}
        raw_tiles, grouped_tiles = {}, {}
        banks, turned_tiles, f_codes, f_scales, accs_0, accs_1 = {}, {}, {}, {}, {}, {}

        def copy_on(on_vector, out, in_):
            if on_vector:
                nc.vector.tensor_copy(out=out, in_=in_)
            else:
                nc.scalar.copy(out=out, in_=in_)

        def interleave(on_vector, grouped, rows):
            copy_on(
                on_vector,
                grouped.rearrange("p (c i j) -> p c j i", i=RUN, j=J),
                rows.rearrange("p j (c i) -> p c j i", i=RUN),
            )

        def quantize(x4, codes, scales, values):
            nc.vector.quantize_mx(out=codes.bitcast(x4), scales=scales, in_=values)

        def store(on_vector, acc, rows):
            result = result_pool.tile([P, W], F32, name="result")
            copy_on(on_vector, result[:], acc[:])
            nc.sync.dma_start(out=rows, in_=result[:])

        def load_gate(out, j, d0, d1, g):
            nc.sync.dma_start(out=out, in_=gates_v[:, d0:d1, j, g * W : (g + 1) * W])

        def new_slot(j):
            c_tiles[j] = slots.tile([P, ND, W], F32, name="c_sb")
            z_tiles[j] = slots.tile([P, ND, W], F32, name="z_sb")
            r_tiles[j] = slots.tile([P, ND, W], F32, name="r_sb")

        def load_x_c(j):
            nc.sync.dma_start(out=x_sb[:, j, :], in_=x_v[:, j, :])
            load_gate(c_tiles[j][:], j, 0, ND, GATE_C)

        def load_z(j):
            load_gate(z_tiles[j][:], j, 0, ND, GATE_Z)

        def load_g_t(j0, j1):
            nc.sync.dma_start(out=g_sb[:, j0:j1, :], in_=g_v[:, j0:j1, :])
            nc.sync.dma_start(out=ds_sb[:, j0:j1, :], in_=t_v[:, j0:j1, :])

        def load_r_hn(j):
            load_gate(r_tiles[j][:], j, 0, ND, GATE_R)
            nc.sync.dma_start(out=hn_sb[:, j, :], in_=hn_v[:, j, :])

        def load_raw(i):
            raw_tiles[i] = grouped_pool.tile([P, J, W], BF16, name="raw")
            nc.sync.dma_start(out=raw_tiles[i][:], in_=wih_v[i] if i < NG else agg_v[i - NG])

        def group_raw(i):
            grouped_tiles[i] = grouped_pool.tile([P, ROW], BF16, name="grouped", align_bytes=64)
            interleave(False, grouped_tiles[i][:], raw_tiles[i][:])

        def quantize_raw(i):
            if i < NG:
                quantize(E4M3X4, wih_codes[:, i, :], wih_scales[:, i, :], grouped_tiles[i][:])
            else:
                quantize(E4M3X4, agg_codes[:, i - NG, :], agg_scales[:, i - NG, :], grouped_tiles[i][:])

        def h_minus_c(j, d0, d1):
            nc.vector.tensor_tensor(
                out=e_tiles[j][:, d0:d1, :],
                in0=x_sb[:, j : j + 1, :].to_broadcast([P, d1 - d0, W]),
                in1=c_tiles[j][:, d0:d1, :],
                op=ALU.subtract,
            )

        def times_z(j, d0, d1):
            nc.vector.tensor_tensor(
                out=e_tiles[j][:, d0:d1, :], in0=z_tiles[j][:, d0:d1, :], in1=e_tiles[j][:, d0:d1, :], op=ALU.mult
            )

        def add_to_hsum(j, term, start, stop):
            nc.tensor.matmul(out=hsum_tiles[j][:], lhsT=ident[:], rhs=term, start=start, stop=stop)

        def start_e(j):
            e_tiles[j] = work.tile([P, ND, W], F32, name="e_sb")
            h_minus_c(j, 0, ND)

        def add_c(j):
            hsum_tiles[j] = acc_pool.tile([P, W], F32, name="acc")
            for d in range(ND):
                add_to_hsum(j, c_tiles[j][:, d, :], d == 0, False)

        def times_z_and_add(j):
            times_z(j, 0, ND)
            for d in range(ND):
                add_to_hsum(j, e_tiles[j][:, d, :], False, d == ND - 1)

        def square_c(j):
            nc.scalar.activation(out=c_tiles[j][:], in_=c_tiles[j][:], func=ACT.Square)

        def square_r(j):
            nc.scalar.activation(out=r_tiles[j][:], in_=r_tiles[j][:], func=ACT.Square, bias=-0.5, scale=1.0)

        def grad_times_t(j0, j1):
            nc.vector.tensor_tensor(out=ds_sb[:, j0:j1, :], in0=g_sb[:, j0:j1, :], in1=ds_sb[:, j0:j1, :], op=ALU.mult)

        def make_ds(j):
            nc.vector.scalar_tensor_tensor(
                out=ds_sb[:, j, :], in0=hsum_tiles[j][:], scalar=0.0, in1=ds_sb[:, j, :], op0=ALU.is_gt, op1=ALU.mult
            )

        def z_minus_1_times_ds(j):
            nc.vector.scalar_tensor_tensor(
                out=z_tiles[j][:], in0=z_tiles[j][:], scalar=1.0, in1=ds_sb[:, j : j + 1, :].to_broadcast([P, ND, W]),
                op0=ALU.subtract, op1=ALU.mult,
            )

        def make_dz(j):
            nc.vector.scalar_tensor_tensor(
                out=d_all[:, DZ, :, j, :], in0=e_tiles[j][:], scalar=-1.0, in1=z_tiles[j][:], op0=ALU.mult, op1=ALU.mult
            )

        def make_dc(j):
            nc.vector.scalar_tensor_tensor(
                out=c_tiles[j][:], in0=c_tiles[j][:], scalar=1.0, in1=z_tiles[j][:], op0=ALU.subtract, op1=ALU.mult
            )

        def round_dc(j):
            nc.scalar.copy(out=d_all[:, DC, :, j, :], in_=c_tiles[j][:])

        def dc_times_r_terms(j):
            nc.vector.scalar_tensor_tensor(
                out=r_tiles[j][:], in0=r_tiles[j][:], scalar=0.25, in1=c_tiles[j][:], op0=ALU.subtract, op1=ALU.mult
            )

        def make_dr(j):
            nc.vector.scalar_tensor_tensor(
                out=d_all[:, DR, :, j, :], in0=r_tiles[j][:], scalar=-1.0,
                in1=hn_sb[:, j : j + 1, :].to_broadcast([P, ND, W]), op0=ALU.mult, op1=ALU.mult,
            )

        def block_words(j, k):
            if k < 2 * ND:
                return d_words[:, k % 2, k // 2, j, :]
            return d_words[:, DR, k - 2 * ND, j, :]

        def blocks_of(b):
            return range(2 * b, min(2 * b + 2, NG * ND))

        def turn(j, b):
            banks[(j, b)] = turn_pool.tile([P, W], F32, name="bank")
            for i, k in enumerate(blocks_of(b)):
                for u in range(2):
                    nc.tensor.transpose(
                        out=banks[(j, b)][:, (2 * i + u) * P : (2 * i + u + 1) * P],
                        in_=block_words(j, k)[:, u : W // 2 : 2],
                        identity=ident[:],
                    )

        def new_turned(j):
            turned_tiles[j] = work.tile([P, NG * ND * W], BF16, name="turned", bufs=1, align_bytes=64)
            f_codes[j] = work.tile([P, NG * ND * P], U32, name="f_codes", align_bytes=64)
            f_scales[j] = work.tile([P, NG * ND * P], U8, name="f_scales", align_bytes=64)

        def copy_turned(j, b):
            n = len(blocks_of(b))
            nc.scalar.copy(
                out=turned_tiles[j][:, 2 * b * W : (2 * b + n) * W].bitcast(F32).rearrange("q (k r u) -> q k r u", k=n, u=2),
                in_=banks[(j, b)][:, 0 : n * 2 * P].rearrange("q (k u r) -> q k r u", k=n, u=2),
            )

        def quantize_turned(j, k0, k1):
            quantize(E5M2X4, f_codes[j][:, k0 * P : k1 * P], f_scales[j][:, k0 * P : k1 * P], turned_tiles[j][:, k0 * W : k1 * W])

        def multiply_0(j):
            for d in range(ND):
                accs_0[(d, j)] = acc_pool.tile([P, W], F32, name="acc")
                for i, (k, g) in enumerate(((2 * d, GATE_C), (2 * d + 1, GATE_Z), (2 * ND + d, GATE_R))):
                    nc.tensor.matmul_mx(
                        out=accs_0[(d, j)][:],
                        lhsT=f_codes[j][:, k * P : (k + 1) * P].bitcast(E5M2X4), lhsT_scale=f_scales[j][:, k * P : (k + 1) * P],
                        rhs=wih_codes[:, g, :].bitcast(E4M3X4), rhs_scale=wih_scales[:, g, :],
                        start=(i == 0), stop=(i == NG - 1),
                    )

        def store_0(j):
            for d in range(ND):
                store(False, accs_0[(d, j)], out0_v[d][:, j, :])

        def rows_of(g, d):
            return d_all[:, DR - g, d, :, :]

        def group_t(on_vector, g, d, m0, m1):
            if m0 == 0:
                grouped_tiles[(g, d)] = grouped_pool.tile([P, ROW], BF16, name="grouped", align_bytes=64)
            interleave(on_vector, grouped_tiles[(g, d)][:, m0 * J * P : m1 * J * P], rows_of(g, d)[:, :, m0 * P : m1 * P])

        def quantize_t(g, d, m0, m1):
            quantize(
                E5M2X4, t_codes[:, g, d, m0 * P : m1 * P], t_scales[:, g, d, m0 * P : m1 * P],
                grouped_tiles[(g, d)][:, m0 * J * P : m1 * J * P],
            )

        def multiply_1(g, m, d0, d1):
            if d0 == 0 and g == GATE_C:
                accs_1[(g, m)] = acc_pool.tile([P, W], F32, name="acc")
            elif d0 == 0:
                accs_1[(g, m)] = turn_pool.tile([P, W], F32, name="bank")
            for d in range(d0, d1):
                nc.tensor.matmul_mx(
                    out=accs_1[(g, m)][:],
                    lhsT=t_codes[:, g, d, m * P : (m + 1) * P].bitcast(E5M2X4), lhsT_scale=t_scales[:, g, d, m * P : (m + 1) * P],
                    rhs=agg_codes[:, d, :].bitcast(E4M3X4), rhs_scale=agg_scales[:, d, :],
                    start=(d == 0), stop=(d == ND - 1),
                )

        def store_1(on_vector, g, m):
            store(on_vector, accs_1[(g, m)], out1_v[g * J + m])

        new_slot(0)
        nc.sync.dma_start(out=x_sb[:, 0, :], in_=x_v[:, 0, :])
        for d in range(ND):
            load_gate(c_tiles[0][:, d : d + 1, :], 0, d, d + 1, GATE_C)
            load_gate(z_tiles[0][:, d : d + 1, :], 0, d, d + 1, GATE_Z)
        new_slot(1)
        load_x_c(1)
        load_g_t(0, 1)
        load_z(1)
        load_raw(0)
        load_r_hn(0)
        new_slot(2)
        load_x_c(2)
        load_raw(1)
        load_g_t(1, J)
        load_z(2)
        load_raw(2)
        load_r_hn(1)

        e_tiles[0] = work.tile([P, ND, W], F32, name="e_sb")
        hsum_tiles[0] = acc_pool.tile([P, W], F32, name="acc")
        h_minus_c(0, 0, 1)
        add_to_hsum(0, c_tiles[0][:, 0, :], True, False)
        h_minus_c(0, 1, 2)
        add_to_hsum(0, c_tiles[0][:, 1, :], False, False)
        times_z(0, 0, 1)
        add_to_hsum(0, e_tiles[0][:, 0, :], False, False)
        h_minus_c(0, 2, 3)
        add_to_hsum(0, c_tiles[0][:, 2, :], False, False)
        times_z(0, 1, 2)
        add_to_hsum(0, e_tiles[0][:, 1, :], False, False)
        times_z(0, 2, 3)
        add_to_hsum(0, e_tiles[0][:, 2, :], False, True)
        start_e(1)
        square_c(0)
        grad_times_t(0, 1)

        spare = [0, 1, 2, 3, 4, 5]

        def use_spare_time(n):
            for i in range(n):
                group_raw(spare.pop(0))

        for j in range(LAST):
            make_ds(j)
            add_c(j + 1)
            if j > 0:
                copy_turned(j - 1, 3)
                copy_turned(j - 1, 4)
                quantize_turned(j - 1, 0, 4)
            z_minus_1_times_ds(j)
            times_z_and_add(j + 1)
            make_dz(j)
            if j > 0:
                quantize_turned(j - 1, 4, 8)
            make_dc(j)
            if j > 0:
                quantize_turned(j - 1, 8, 9)
            if j == 2:
                multiply_0(j - 1)
            use_spare_time(SPARE_A[j])
            square_r(j)
            square_c(j + 1)
            use_spare_time(SPARE_B[j])
            round_dc(j)
            new_turned(j)
            for b in range(3):
                turn(j, b)
            if j + 2 < J:
                start_e(j + 2)
            dc_times_r_terms(j)
            if j == 0:
                grad_times_t(1, J)
            else:
                quantize_raw(3 * (j - 1))
            make_dr(j)
            use_spare_time(SPARE_C[j])
            if j == 2:
                store_0(j - 1)
            for b in range(3):
                copy_turned(j, b)
            turn(j, 3)
            turn(j, 4)
            if j == 0:
                new_slot(LAST)
                load_x_c(LAST)
                load_z(LAST)
                load_r_hn(2)
                load_raw(3)
                load_raw(4)
                load_raw(5)
                load_r_hn(LAST)
            if j == 1:
                quantize_raw(1)
                quantize_raw(2)
                use_spare_time(1)
                multiply_0(0)
                store_0(0)
            if j == 2:
                quantize_raw(4)

        make_ds(LAST)
        copy_turned(LAST - 1, 3)
        copy_turned(LAST - 1, 4)
        quantize_turned(LAST - 1, 0, 4)
        z_minus_1_times_ds(LAST)
        quantize_turned(LAST - 1, 4, 8)
        make_dc(LAST)
        square_r(LAST)
        round_dc(LAST)
        quantize_turned(LAST - 1, 8, 9)
        make_dz(LAST)
        multiply_0(LAST - 1)
        new_turned(LAST)
        for b in range(3):
            turn(LAST, b)
        dc_times_r_terms(LAST)
        group_t(False, GATE_C, 0, 0, J)
        quantize_raw(5)
        make_dr(LAST)
        store_0(LAST - 1)
        for b in range(3):
            copy_turned(LAST, b)
        turn(LAST, 3)
        turn(LAST, 4)
        copy_turned(LAST, 3)
        copy_turned(LAST, 4)
        group_t(True, GATE_Z, 0, 0, J)
        group_t(True, GATE_Z, 1, 0, J)
        quantize_turned(LAST, 0, 4)
        quantize_turned(LAST, 4, 8)
        quantize_turned(LAST, 8, 9)
        multiply_0(LAST)
        quantize_t(GATE_C, 0, 0, J)
        group_t(False, GATE_C, 1, 0, J)
        quantize_t(GATE_Z, 0, 0, J)
        group_t(True, GATE_Z, 2, 0, J)
        quantize_t(GATE_Z, 1, 0, J)
        quantize_t(GATE_Z, 2, 0, J)
        for d in range(ND):
            for m in range(J):
                multiply_1(GATE_Z, m, d, d + 1)
        group_t(False, GATE_C, 2, 0, J)
        quantize_t(GATE_C, 1, 0, J)
        group_t(True, GATE_R, 0, 0, J)
        quantize_t(GATE_C, 2, 0, J)
        store_0(LAST)
        for m in range(J):
            multiply_1(GATE_C, m, 0, ND)
        for m in range(J):
            store_1(False, GATE_Z, m)
        group_t(True, GATE_R, 1, 0, J)
        quantize_t(GATE_R, 0, 0, J)
        group_t(True, GATE_R, 2, 0, 1)
        quantize_t(GATE_R, 1, 0, J)
        for m in range(J):
            store_1(False, GATE_C, m)
        group_t(True, GATE_R, 2, 1, 2)
        for m in range(J):
            quantize_t(GATE_R, 2, m, m + 1)
            if m + 2 < J:
                group_t(True, GATE_R, 2, m + 2, m + 3)
            multiply_1(GATE_R, m, 0, ND)
            if m < LAST:
                store_1(False, GATE_R, m)
        store_1(True, GATE_R, LAST)
